import numpy as np
import ml_dtypes


def mxq(x, axis, fmt="e4m3"):
    dtype, down = {"e4m3": (ml_dtypes.float8_e4m3fn, 7), "e5m2": (ml_dtypes.float8_e5m2, 14)}[fmt]
    v = np.moveaxis(np.asarray(x, np.float32).astype(ml_dtypes.bfloat16).astype(np.float64), axis, -1)
    blocks = v.reshape(v.shape[:-1] + (-1, 32))
    amax = np.abs(blocks).max(-1, keepdims=True)
    byte = np.maximum(np.where(amax > 0, np.frexp(amax)[1] - 1 + 127, 0) - down, 1)
    scale = np.exp2(byte - 127.0)
    codes = (blocks / scale).astype(np.float32).astype(dtype).astype(np.float64)
    return np.moveaxis((codes * scale).reshape(v.shape), -1, axis)


WIDE = False


def mx_kscale(k):
    if not WIDE:
        return np.ones(k)
    levels = np.array([10, -10, 5, -5, 0])
    if k % 512:
        return np.exp2(np.random.permutation(np.resize(levels, k // 32))).repeat(32)
    a = np.empty((k // 512, 16))
    for p in range(k // 512):
        a[p, :8] = np.random.permutation(np.resize(levels, 8))
        for g in range(8):
            far = levels[np.abs(levels - a[p, g]) >= 10]
            a[p, g + 8] = far[np.random.randint(len(far))]
    return np.exp2(a.ravel()).repeat(32)


BF16 = ml_dtypes.bfloat16


def bf(x):
    return np.asarray(x, np.float32).astype(BF16)


def f64(x):
    return np.asarray(x).astype(np.float64)


B, S, D, H, KVH, HD = 1, 512, 2048, 16, 4, 128
E = H * HD
KV = KVH * HD
EPS = 1e-6


def layernorm(u, gamma, beta):
    mu = u.mean(-1, keepdims=True)
    var = np.square(u - mu).mean(-1, keepdims=True)
    return (u - mu) / np.sqrt(var + EPS) * gamma + beta


def apply_rope(u, cos, sin):
    half = u.shape[-1] // 2
    rotated = np.concatenate([-u[..., half:], u[..., :half]], axis=-1)
    return u * cos[None, None] + rotated * sin[None, None]


def draw0():
    s = mx_kscale(D)
    return {
        "x": bf(np.random.standard_normal((B, S, D)) * s),
        "cos": bf(np.random.uniform(size=(S, HD))),
        "sin": bf(np.random.uniform(size=(S, HD))),
        "Wq": bf(np.random.standard_normal((D, E)) / np.sqrt(D) / s[:, None]),
        "Wk": bf(np.random.standard_normal((D, KV)) / np.sqrt(D) / s[:, None]),
        "Wv": bf(np.random.standard_normal((D, KV)) * 2.0 / np.sqrt(D) / s[:, None]),
        "q_gamma": bf(1.0 + 0.1 * np.random.standard_normal(HD)),
        "q_beta": bf(0.1 * np.random.standard_normal(HD)),
        "k_gamma": bf(1.0 + 0.1 * np.random.standard_normal(HD)),
        "k_beta": bf(0.1 * np.random.standard_normal(HD)),
    }


def core(x, cos, sin, Wq, Wk, Wv, q_gamma, q_beta, k_gamma, k_beta):
    xq = mxq(f64(x), 2, "e4m3")
    q = (xq @ mxq(f64(Wq), 0, "e4m3")).reshape(B, S, H, HD).transpose(0, 2, 1, 3)
    k = (xq @ mxq(f64(Wk), 0, "e4m3")).reshape(B, S, KVH, HD).transpose(0, 2, 1, 3)
    v = (xq @ mxq(f64(Wv), 0, "e4m3")).reshape(B, S, KVH, HD).transpose(0, 2, 1, 3)
    q = layernorm(q, f64(q_gamma), f64(q_beta))
    k = layernorm(k, f64(k_gamma), f64(k_beta))
    q_rot = apply_rope(q, f64(cos), f64(sin))
    k_rot = apply_rope(k, f64(cos), f64(sin))
    return q_rot, k_rot, v


def e4m3fn_bytes(y):
    return np.clip(np.asarray(y, np.float64), -448.0, 448.0).astype(np.float32).astype(ml_dtypes.float8_e4m3fn).view(np.uint8)


def e4m3fn_values(b):
    return np.asarray(b, np.uint8).view(ml_dtypes.float8_e4m3fn).astype(np.float64)


def setup_inputs():
    d = draw0()
    x0 = np.asarray(d['Wq']).astype(np.float64)
    s = (np.max(np.abs(x0), axis=(1,), keepdims=True) / 448.0).astype(np.float32)
    out = {}
    for k, v in d.items():
        if k == 'Wq':
            out['Wq_bytes'] = e4m3fn_bytes(x0 / s.astype(np.float64))
            out['Wq_scale'] = s
        else:
            out[k] = v
    return out


def reference(x, cos, sin, Wq_bytes, Wq_scale, Wk, Wv, q_gamma, q_beta, k_gamma, k_beta):
    return core(x, cos, sin, e4m3fn_values(Wq_bytes) * Wq_scale.astype(np.float64), Wk, Wv, q_gamma, q_beta, k_gamma, k_beta)

@@ -1,0 +1,363 @@
+from contextlib import ExitStack
+
+import concourse.mybir as mybir
+from concourse.masks import make_identity
+
+F32 = mybir.dt.float32
+BF16 = mybir.dt.bfloat16
+U32 = mybir.dt.uint32
+U8 = mybir.dt.uint8
+FP8 = mybir.dt.float8_e4m3fn
+FP8X4 = mybir.dt.float8_e4m3fn_x4
+ALU = mybir.AluOpType
+ACT = mybir.ActivationFunctionType
+
+P = 128
+HD = 128
+HALF = 64
+NT = 4
+NG = 4
+GW = 512
+EPS = 1e-6
+FLOPS = 2 * 512 * 2048 * 3072
+
+GROUPS = (("q", 0), ("q", 1), ("k", 0), ("q", 2), ("q", 3), ("v", 0))
+NCHUNK = 24
+DS = 5
+DV = 6
+
+
+def weave(segs, fill):
+    ops = []
+    n = len(fill)
+    k = 0
+    for seg in segs:
+        ops.extend(seg)
+        ops.extend(fill[(k * n + 3) // 4 : ((k + 1) * n + 3) // 4])
+        k += 1
+    return ops
+
+
+def tile_gqa_flashattn_pa_kernel(
+    tc, x, cos, sin, wq_bytes, wq_scale, wk, wv, q_gamma, q_beta, k_gamma, k_beta, out_q, out_k, out_v
+):
+    nc = tc.nc
+    with ExitStack() as ctx:
+        const = ctx.enter_context(tc.tile_pool(name="const", bufs=1))
+        bytes_pool = ctx.enter_context(tc.tile_pool(name="bytes", bufs=16))
+        raw_pool = ctx.enter_context(tc.tile_pool(name="raw", bufs=8))
+        x_pool = ctx.enter_context(tc.tile_pool(name="xraw", bufs=4))
+        gx_pool = ctx.enter_context(tc.tile_pool(name="gx", bufs=8))
+        wide_pool = ctx.enter_context(tc.tile_pool(name="wide", bufs=3))
+        grp_pool = ctx.enter_context(tc.tile_pool(name="grp", bufs=3))
+        code_pool = ctx.enter_context(tc.tile_pool(name="codes", bufs=4))
+        stat_pool = ctx.enter_context(tc.tile_pool(name="stats", bufs=4))
+        junk_pool = ctx.enter_context(tc.tile_pool(name="junk", bufs=4))
+        ab_pool = ctx.enter_context(tc.tile_pool(name="ab", bufs=2))
+        c_pool = ctx.enter_context(tc.tile_pool(name="cc", bufs=2))
+        o_pool = ctx.enter_context(tc.tile_pool(name="o", bufs=4))
+        psum = ctx.enter_context(tc.psum_pool(name="psum", bufs=1))
+        ctx.enter_context(tc.manual_schedule())
+
+        ident = const.tile([P, P], F32, name="ident", tag="ident")
+        make_identity(nc, ident[:])
+        one = const.tile([P, 1], F32, name="one", tag="one")
+        nc.gpsimd.memset(one[:], 1.0)
+        warm = const.tile([P, 1], F32, name="warm", tag="warm")
+        nc.scalar.activation(out=warm[:], in_=one[:], func=ACT.Sqrt)
+
+        wsc = const.tile([P, NG * 4], F32, name="wsc", tag="wsc")
+        nc.sync.dma_start(
+            out=wsc[:].rearrange("p (g t) -> p g t", g=NG),
+            in_=wq_scale.rearrange("(g p t) o -> p g (t o)", p=P, t=4),
+        )
+        wq_v = wq_bytes.rearrange("(g p t) n -> g p t n", p=P, t=4)
+        wk_v = wk.rearrange("(g p t) n -> g p t n", p=P, t=4)
+        wv_v = wv.rearrange("(g p t) n -> g p t n", p=P, t=4)
+        raw = {}
+        xr = {}
+
+        def load_chunk(s):
+            kind, idx = GROUPS[s // NG]
+            g = s % NG
+            if kind == "q":
+                t = bytes_pool.tile([P, 4, GW], U8, name="wq_bytes", tag="wq_bytes")
+                nc.sync.dma_start(out=t[:], in_=wq_v[g][:, :, idx * GW : (idx + 1) * GW])
+            else:
+                t = raw_pool.tile([P, 4, GW], BF16, name="wkv_raw", tag="wkv_raw")
+                nc.sync.dma_start(out=t[:], in_=(wk_v if kind == "k" else wv_v)[g])
+            raw[s] = t
+
+        def load_x(i):
+            t = x_pool.tile([P, 2048], BF16, name="xraw", tag="xraw")
+            nc.sync.dma_start(out=t[:], in_=x[0, i * P : (i + 1) * P, :])
+            xr[i] = t
+
+        load_chunk(0)
+        load_chunk(1)
+        load_x(0)
+        load_x(1)
+        load_chunk(2)
+        load_x(2)
+        load_x(3)
+        load_chunk(3)
+        cs = const.tile([P, 2, NT, HD], BF16, name="cs", tag="cs")
+        nc.sync.dma_start(out=cs[:, 0, :, :], in_=cos.rearrange("(i p) d -> p i d", p=P))
+        nc.sync.dma_start(out=cs[:, 1, :, :], in_=sin.rearrange("(i p) d -> p i d", p=P))
+        gb = const.tile([P, 4, HD], BF16, name="gb", tag="gb")
+        v = 0
+        for vec in (q_gamma, q_beta, k_gamma, k_beta):
+            nc.sync.dma_start(out=gb[:, v, :], in_=vec.partition_broadcast(P))
+            v += 1
+        for s in range(4, NCHUNK):
+            load_chunk(s)
+
+        xc = const.tile([P, NT * NG * P], U32, name="xc", tag="xc", align_bytes=64)
+        xs = const.tile([P, NT * NG * P], U8, name="xs", tag="xs", align_bytes=64)
+        gxs = {}
+
+        def x_turn(i):
+            words = xr[i][:].bitcast(F32)
+            for half in range(2):
+                xt = psum.tile([P, 2, 2, P], F32, name="xt", tag="bank%d" % ((2 * i + half) % 8))
+                for gl in range(2):
+                    g = 2 * half + gl
+                    for u in range(2):
+                        nc.tensor.transpose(xt[:, gl, u, :], words[:, 256 * g + u : 256 * (g + 1) : 2], ident[:])
+                gx = gx_pool.tile([P, 2, P, 4], BF16, name="gx", tag="gx", align_bytes=64)
+                dst = gx[:].rearrange("p g r j -> p (g r j)").bitcast(F32).rearrange("p (g r u) -> p g r u", g=2, u=2)
+                src = xt[:].rearrange("p g u r -> p g r u")
+                if half == 0:
+                    nc.scalar.copy(out=dst, in_=src)
+                else:
+                    nc.vector.tensor_copy(out=dst, in_=src)
+                gxs[(i, half)] = gx
+
+        def x_quant(i):
+            for half in range(2):
+                lo = (NG * i + 2 * half) * P
+                nc.vector.quantize_mx(
+                    out=xc[:, lo : lo + 2 * P].bitcast(FP8X4),
+                    scales=xs[:, lo : lo + 2 * P],
+                    in_=gxs[(i, half)][:].rearrange("p g r j -> p (g r j)"),
+                )
+
+        tabs = {}
+
+        def build_tables():
+            cosv = cs[:, 0, :, :]
+            sinv = cs[:, 1, :, :]
+            w = 0
+            for kind in ("q", "k"):
+                gam = gb[:, 2 * w, :]
+                bet = gb[:, 2 * w + 1, :]
+                ab_t = const.tile([P, NT, 2, HD], F32, name="abt_" + kind, tag="abt_" + kind)
+                c_t = const.tile([P, NT, HD], F32, name="ct_" + kind, tag="ct_" + kind)
+                tmp = const.tile([P, NT, HD], F32, name="tmp_" + kind, tag="tmp_" + kind)
+
+                def bc(ap, width):
+                    return ap.unsqueeze(1).to_broadcast([P, NT, width])
+
+                nc.vector.tensor_tensor(out=ab_t[:, :, 0, :], in0=cosv, in1=bc(gam, HD), op=ALU.mult)
+                nc.vector.tensor_tensor(
+                    out=ab_t[:, :, 1, 0:HALF], in0=sinv[:, :, HALF:HD], in1=bc(gam[:, 0:HALF], HALF), op=ALU.mult
+                )
+                nc.vector.scalar_tensor_tensor(
+                    out=ab_t[:, :, 1, HALF:HD], in0=sinv[:, :, 0:HALF], scalar=-1.0, in1=bc(gam[:, HALF:HD], HALF),
+                    op0=ALU.mult, op1=ALU.mult,
+                )
+                nc.vector.tensor_tensor(out=c_t[:], in0=cosv, in1=bc(bet, HD), op=ALU.mult)
+                nc.vector.scalar_tensor_tensor(
+                    out=tmp[:, :, 0:HALF], in0=sinv[:, :, 0:HALF], scalar=-1.0, in1=bc(bet[:, HALF:HD], HALF),
+                    op0=ALU.mult, op1=ALU.mult,
+                )
+                nc.vector.tensor_tensor(
+                    out=tmp[:, :, HALF:HD], in0=sinv[:, :, HALF:HD], in1=bc(bet[:, 0:HALF], HALF), op=ALU.mult
+                )
+                nc.vector.tensor_tensor(out=c_t[:], in0=c_t[:], in1=tmp[:], op=ALU.add)
+                tabs[kind] = (ab_t, c_t)
+                w += 1
+
+        wides = {}
+        grps = {}
+        codes = {}
+        accs = {}
+
+        def widen_plane(s, t):
+            def run():
+                g = s % NG
+                nc.scalar.activation(
+                    out=wides[s][:, t, :], in_=raw[s][:, t, :].bitcast(FP8), func=ACT.Copy,
+                    scale=wsc[:, 4 * g + t : 4 * g + t + 1],
+                )
+            return run
+
+        def scalar_interleave(s, part):
+            def run():
+                lo = part * (GW // 2)
+                hi = lo + GW // 2
+                nc.scalar.copy(out=grps[s][:, lo:hi, :], in_=raw[s][:, :, lo:hi].rearrange("p t n -> p n t"))
+            return run
+
+        def prep_scalar_ops(s):
+            kind = GROUPS[s // NG][0]
+            if kind == "q":
+                wides[s] = wide_pool.tile([P, 4, GW], BF16, name="wide", tag="wide")
+                return [widen_plane(s, t) for t in range(4)]
+            grps[s] = grp_pool.tile([P, GW, 4], BF16, name="grp", tag="grp", align_bytes=64)
+            return [scalar_interleave(s, part) for part in range(2)]
+
+        def interleave(s):
+            if GROUPS[s // NG][0] == "q":
+                grps[s] = grp_pool.tile([P, GW, 4], BF16, name="grp", tag="grp", align_bytes=64)
+                nc.vector.tensor_copy(out=grps[s][:], in_=wides[s][:].rearrange("p t n -> p n t"))
+
+        def quantize(s):
+            wc = code_pool.tile([P, GW], U32, name="wc", tag="wc", align_bytes=64)
+            ws = code_pool.tile([P, GW], U8, name="ws", tag="ws", align_bytes=64)
+            nc.vector.quantize_mx(
+                out=wc[:].bitcast(FP8X4), scales=ws[:], in_=grps[s][:].rearrange("p n t -> p (n t)")
+            )
+            codes[s] = (wc, ws)
+
+        def multiply(s):
+            c = s // NG
+            g = s % NG
+            if g == 0:
+                for i in range(NT):
+                    accs[(c, i)] = psum.tile([P, GW], F32, name="acc", tag="bank%d" % ((c % 2) * NT + i))
+            wc, ws = codes[s]
+            for i in range(NT):
+                lo = (NG * i + g) * P
+                nc.tensor.matmul_mx(
+                    out=accs[(c, i)][:],
+                    lhsT=xc[:, lo : lo + P].bitcast(FP8X4),
+                    lhsT_scale=xs[:, lo : lo + P],
+                    rhs=wc[:].bitcast(FP8X4),
+                    rhs_scale=ws[:],
+                    start=(g == 0),
+                    stop=(g == NG - 1),
+                )
+
+        stats = {}
+        work = {}
+
+        def stats_segments(e):
+            c = e // NT
+            i = e % NT
+            acc = accs[(c, i)]
+            st = stat_pool.tile([P, 16], F32, name="st", tag="st")
+            stats[e] = st
+
+            def head_sum(h):
+                def run():
+                    junk = junk_pool.tile([P, HD], BF16, name="junk", tag="junk")
+                    nc.scalar.activation(
+                        out=junk[:], in_=acc[:, h * HD : (h + 1) * HD], func=ACT.Identity, accum_out=st[:, h : h + 1]
+                    )
+                return run
+
+            def neg_mean():
+                nc.scalar.activation(out=st[:, 4:8], in_=st[:, 0:4], func=ACT.Copy, scale=-1.0 / HD)
+
+            def head_sq(h):
+                def run():
+                    junk = junk_pool.tile([P, HD], BF16, name="junk", tag="junk")
+                    nc.scalar.activation(
+                        out=junk[:], in_=acc[:, h * HD : (h + 1) * HD], func=ACT.Square,
+                        bias=st[:, 4 + h : 5 + h], accum_out=st[:, 8 + h : 9 + h],
+                    )
+                return run
+
+            def std():
+                nc.scalar.activation(out=st[:, 12:16], in_=st[:, 8:12], func=ACT.Sqrt, scale=1.0 / HD, bias=EPS)
+
+            return [[head_sum(h) for h in range(4)], [neg_mean], [head_sq(h) for h in range(4)], [std]]
+
+        def epi_ab(e):
+            c = e // NT
+            i = e % NT
+            kind = GROUPS[c][0]
+            acc = accs[(c, i)]
+            st = stats[e]
+            rt = stat_pool.tile([P, 4], F32, name="rt", tag="rt")
+            nc.vector.reciprocal(out=rt[:], in_=st[:, 12:16])
+            ab = ab_pool.tile([P, 4, 2, HD], F32, name="ab", tag="ab")
+            for h in range(4):
+                nc.vector.scalar_tensor_tensor(
+                    out=ab[:, h, :, :],
+                    in0=acc[:, h * HD : (h + 1) * HD].unsqueeze(1).to_broadcast([P, 2, HD]),
+                    scalar=st[:, 4 + h : 5 + h],
+                    in1=tabs[kind][0][:, i, :, :],
+                    op0=ALU.add,
+                    op1=ALU.mult,
+                )
+            work[e] = (ab, rt)
+
+        def out_view(c, i):
+            kind, idx = GROUPS[c]
+            dram = out_q if kind == "q" else (out_k if kind == "k" else out_v)
+            return dram[0, 4 * idx : 4 * idx + 4, i * P : (i + 1) * P, :].rearrange("h p d -> p h d")
+
+        def epi_rest(e):
+            c = e // NT
+            i = e % NT
+            kind = GROUPS[c][0]
+            ab, rt = work[e]
+            cc = c_pool.tile([P, 4, HD], F32, name="cc", tag="cc")
+            nc.vector.tensor_tensor(out=cc[:, :, 0:HALF], in0=ab[:, :, 0, 0:HALF], in1=ab[:, :, 1, HALF:HD], op=ALU.add)
+            nc.vector.tensor_tensor(out=cc[:, :, HALF:HD], in0=ab[:, :, 0, HALF:HD], in1=ab[:, :, 1, 0:HALF], op=ALU.add)
+            o = o_pool.tile([P, 4, HD], F32, name="o", tag="o")
+            for h in range(4):
+                nc.vector.scalar_tensor_tensor(
+                    out=o[:, h, :], in0=cc[:, h, :], scalar=rt[:, h : h + 1], in1=tabs[kind][1][:, i, :],
+                    op0=ALU.mult, op1=ALU.add,
+                )
+            nc.sync.dma_start(out=out_view(c, i), in_=o[:])
+
+        def copy_values(c):
+            for i in range(NT):
+                o = o_pool.tile([P, 4, HD], F32, name="o", tag="o")
+                flat = o[:].rearrange("p h d -> p (h d)")
+                if i % 2 == 0:
+                    nc.scalar.copy(out=flat, in_=accs[(c, i)][:])
+                else:
+                    nc.vector.tensor_copy(out=flat, in_=accs[(c, i)][:])
+                nc.sync.dma_start(out=out_view(c, i), in_=o[:])
+
+        def normed(e):
+            return 0 <= e < NCHUNK and GROUPS[e // NT][0] != "v"
+
+        for s in range(NCHUNK + DV + 1):
+            fill = prep_scalar_ops(s) if s < NCHUNK else []
+            segs = stats_segments(s - DS) if normed(s - DS) else [[], [], [], []]
+            for op in weave(segs, fill):
+                op()
+            if s == 0:
+                x_turn(0)
+                x_turn(1)
+            if s == 1:
+                x_turn(2)
+                x_turn(3)
+            if 1 <= s <= NCHUNK:
+                interleave(s - 1)
+            if s == 1:
+                x_quant(0)
+                x_quant(1)
+            if s == 2:
+                x_quant(2)
+                x_quant(3)
+            if s == 4:
+                build_tables()
+            if normed(s - DV):
+                epi_ab(s - DV)
+            if 1 <= s <= NCHUNK:
+                quantize(s - 1)
+            if s == 2:
+                multiply(0)
+            if 2 <= s <= NCHUNK:
+                multiply(s - 1)
+            if normed(s - DV):
+                epi_rest(s - DV)
+            if s >= 5 and (s - 5) % NG == 0 and (s - 5) // NG < len(GROUPS) and GROUPS[(s - 5) // NG][0] == "v":
+                copy_values((s - 5) // NG)

@@ -21,21 +21,12 @@ GW = 512
 EPS = 1e-6
 FLOPS = 2 * 512 * 2048 * 3072
 
-GROUPS = (("q", 0), ("q", 1), ("k", 0), ("q", 2), ("q", 3), ("v", 0))
+GROUPS = (("q", 0), ("q", 1), ("q", 2), ("q", 3), ("k", 0), ("v", 0))
 NCHUNK = 24
-DS = 5
-DV = 6
-
-
-def weave(segs, fill):
-    ops = []
-    n = len(fill)
-    k = 0
-    for seg in segs:
-        ops.extend(seg)
-        ops.extend(fill[(k * n + 3) // 4 : ((k + 1) * n + 3) // 4])
-        k += 1
-    return ops
+NNORM = 20
+SA = 2
+S_INTER = (20, 21, 22, 23)
+PE_ADD = 18
 
 
 def tile_gqa_flashattn_pa_kernel(
@@ -48,23 +39,34 @@ def tile_gqa_flashattn_pa_kernel(
         raw_pool = ctx.enter_context(tc.tile_pool(name="raw", bufs=8))
         x_pool = ctx.enter_context(tc.tile_pool(name="xraw", bufs=4))
         gx_pool = ctx.enter_context(tc.tile_pool(name="gx", bufs=8))
-        wide_pool = ctx.enter_context(tc.tile_pool(name="wide", bufs=3))
-        grp_pool = ctx.enter_context(tc.tile_pool(name="grp", bufs=3))
-        code_pool = ctx.enter_context(tc.tile_pool(name="codes", bufs=4))
+        wide_pool = ctx.enter_context(tc.tile_pool(name="wide", bufs=6))
+        grp_pool = ctx.enter_context(tc.tile_pool(name="grp", bufs=5))
+        code_pool = ctx.enter_context(tc.tile_pool(name="codes", bufs=10))
         stat_pool = ctx.enter_context(tc.tile_pool(name="stats", bufs=4))
         junk_pool = ctx.enter_context(tc.tile_pool(name="junk", bufs=4))
-        ab_pool = ctx.enter_context(tc.tile_pool(name="ab", bufs=2))
+        ab_pool = ctx.enter_context(tc.tile_pool(name="ab", bufs=3))
         c_pool = ctx.enter_context(tc.tile_pool(name="cc", bufs=2))
         o_pool = ctx.enter_context(tc.tile_pool(name="o", bufs=4))
         psum = ctx.enter_context(tc.psum_pool(name="psum", bufs=1))
         ctx.enter_context(tc.manual_schedule())
 
-        ident = const.tile([P, P], F32, name="ident", tag="ident")
-        make_identity(nc, ident[:])
         one = const.tile([P, 1], F32, name="one", tag="one")
         nc.gpsimd.memset(one[:], 1.0)
         warm = const.tile([P, 1], F32, name="warm", tag="warm")
         nc.scalar.activation(out=warm[:], in_=one[:], func=ACT.Sqrt)
+        rmat = const.tile([P, 4, P], BF16, name="rmat", tag="rmat")
+        make_identity(nc, rmat[:, 1, :])
+        nc.gpsimd.tensor_copy(out=rmat[:, 2, :], in_=rmat[:, 1, :])
+        nc.gpsimd.tensor_copy(out=rmat[:, 0, 0:HALF], in_=rmat[:, 1, 0:HALF])
+        nc.gpsimd.tensor_scalar(
+            out=rmat[:, 0, HALF:P], in0=rmat[:, 1, HALF:P], scalar1=-1.0, scalar2=0.0, op0=ALU.mult, op1=ALU.add
+        )
+        nc.gpsimd.tensor_scalar(
+            out=rmat[:, 3, 0:HALF], in0=rmat[:, 1, HALF:P], scalar1=-1.0, scalar2=0.0, op0=ALU.mult, op1=ALU.add
+        )
+        nc.gpsimd.tensor_copy(out=rmat[:, 3, HALF:P], in_=rmat[:, 1, 0:HALF])
+        ident = const.tile([P, P], F32, name="ident", tag="ident")
+        make_identity(nc, ident[:])
 
         wsc = const.tile([P, NG * 4], F32, name="wsc", tag="wsc")
         nc.sync.dma_start(
@@ -94,44 +96,77 @@ def tile_gqa_flashattn_pa_kernel(
             xr[i] = t
 
         load_chunk(0)
+        gcol = const.tile([P, 4, 16], BF16, name="gcol", tag="gcol")
+        v = 0
+        with nc.allow_non_contiguous_dma(reason="four vectors of 128 values, one value to a partition"):
+            for vec in (q_gamma, q_beta, k_gamma, k_beta):
+                nc.sync.dma_start(out=gcol[:, v, 0:1], in_=vec.rearrange("(p o) -> p o", o=1))
+                v += 1
+        cs3 = const.tile([P, NT, 3, HD], BF16, name="cs3", tag="cs3")
+        cos_v = cos.rearrange("(i p) d -> p i d", p=P)
+        sin_v = sin.rearrange("(i p) d -> p i d", p=P)
+        nc.sync.dma_start(out=cs3[:, :, 1, :], in_=cos_v)
+        nc.sync.dma_start(out=cs3[:, :, 2, :], in_=sin_v)
+        nc.sync.dma_start(out=cs3[:, :, 0, 0:HALF], in_=sin_v[:, :, HALF:HD])
+        nc.sync.dma_start(out=cs3[:, :, 0, HALF:HD], in_=sin_v[:, :, 0:HALF])
         load_chunk(1)
         load_x(0)
-        load_x(1)
         load_chunk(2)
-        load_x(2)
-        load_x(3)
+        load_x(1)
         load_chunk(3)
-        cs = const.tile([P, 2, NT, HD], BF16, name="cs", tag="cs")
-        nc.sync.dma_start(out=cs[:, 0, :, :], in_=cos.rearrange("(i p) d -> p i d", p=P))
-        nc.sync.dma_start(out=cs[:, 1, :, :], in_=sin.rearrange("(i p) d -> p i d", p=P))
-        gb = const.tile([P, 4, HD], BF16, name="gb", tag="gb")
-        v = 0
-        for vec in (q_gamma, q_beta, k_gamma, k_beta):
-            nc.sync.dma_start(out=gb[:, v, :], in_=vec.partition_broadcast(P))
-            v += 1
-        for s in range(4, NCHUNK):
+        load_x(2)
+        load_chunk(4)
+        load_x(3)
+        for s in range(5, NCHUNK):
             load_chunk(s)
+
+        gps = {}
+        w = 0
+        for kind in ("q", "k"):
+            gp = psum.tile([P, 2, 2 * HD], F32, name="gps", tag="b%d" % (6 + w))
+            for j in range(2):
+                nc.tensor.matmul(
+                    out=gp[:, j, :],
+                    lhsT=gcol[:, 2 * w + j, 0:1].to_broadcast([P, P]),
+                    rhs=rmat[:, 2 * j : 2 * j + 2, :],
+                    start=True,
+                    stop=True,
+                )
+            gps[kind] = gp
+            w += 1
+        tabs = {}
+
+        def build_tables(kind):
+            gp = gps[kind]
+
+            def bc(j):
+                return gp[:, j, :].rearrange("p (w d) -> p w d", w=2).unsqueeze(1).to_broadcast([P, NT, 2, HD])
+
+            ab_t = const.tile([P, NT, 2, HD], F32, name="abt_" + kind, tag="abt_" + kind)
+            c_t = const.tile([P, NT, HD], F32, name="ct_" + kind, tag="ct_" + kind)
+            tmp = const.tile([P, NT, 2, HD], F32, name="tmp", tag="tmp")
+            nc.vector.tensor_tensor(out=ab_t[:], in0=cs3[:, :, 0:2, :], in1=bc(0), op=ALU.mult)
+            nc.vector.tensor_tensor(out=tmp[:], in0=cs3[:, :, 1:3, :], in1=bc(1), op=ALU.mult)
+            nc.vector.tensor_tensor(out=c_t[:], in0=tmp[:, :, 0, :], in1=tmp[:, :, 1, :], op=ALU.add)
+            tabs[kind] = (ab_t, c_t)
 
         xc = const.tile([P, NT * NG * P], U32, name="xc", tag="xc", align_bytes=64)
         xs = const.tile([P, NT * NG * P], U8, name="xs", tag="xs", align_bytes=64)
         gxs = {}
 
-        def x_turn(i):
-            words = xr[i][:].bitcast(F32)
-            for half in range(2):
-                xt = psum.tile([P, 2, 2, P], F32, name="xt", tag="bank%d" % ((2 * i + half) % 8))
+        def x_turn(i, half):
+            def run():
+                words = xr[i][:].bitcast(F32)
+                xt = psum.tile([P, 2, 2, P], F32, name="xt", tag="b%d" % (2 * i + half))
                 for gl in range(2):
                     g = 2 * half + gl
                     for u in range(2):
                         nc.tensor.transpose(xt[:, gl, u, :], words[:, 256 * g + u : 256 * (g + 1) : 2], ident[:])
                 gx = gx_pool.tile([P, 2, P, 4], BF16, name="gx", tag="gx", align_bytes=64)
                 dst = gx[:].rearrange("p g r j -> p (g r j)").bitcast(F32).rearrange("p (g r u) -> p g r u", g=2, u=2)
-                src = xt[:].rearrange("p g u r -> p g r u")
-                if half == 0:
-                    nc.scalar.copy(out=dst, in_=src)
-                else:
-                    nc.vector.tensor_copy(out=dst, in_=src)
+                nc.scalar.copy(out=dst, in_=xt[:].rearrange("p g u r -> p g r u"))
                 gxs[(i, half)] = gx
+            return run
 
         def x_quant(i):
             for half in range(2):
@@ -142,46 +177,9 @@ def tile_gqa_flashattn_pa_kernel(
                     in_=gxs[(i, half)][:].rearrange("p g r j -> p (g r j)"),
                 )
 
-        tabs = {}
-
-        def build_tables():
-            cosv = cs[:, 0, :, :]
-            sinv = cs[:, 1, :, :]
-            w = 0
-            for kind in ("q", "k"):
-                gam = gb[:, 2 * w, :]
-                bet = gb[:, 2 * w + 1, :]
-                ab_t = const.tile([P, NT, 2, HD], F32, name="abt_" + kind, tag="abt_" + kind)
-                c_t = const.tile([P, NT, HD], F32, name="ct_" + kind, tag="ct_" + kind)
-                tmp = const.tile([P, NT, HD], F32, name="tmp_" + kind, tag="tmp_" + kind)
-
-                def bc(ap, width):
-                    return ap.unsqueeze(1).to_broadcast([P, NT, width])
-
-                nc.vector.tensor_tensor(out=ab_t[:, :, 0, :], in0=cosv, in1=bc(gam, HD), op=ALU.mult)
-                nc.vector.tensor_tensor(
-                    out=ab_t[:, :, 1, 0:HALF], in0=sinv[:, :, HALF:HD], in1=bc(gam[:, 0:HALF], HALF), op=ALU.mult
-                )
-                nc.vector.scalar_tensor_tensor(
-                    out=ab_t[:, :, 1, HALF:HD], in0=sinv[:, :, 0:HALF], scalar=-1.0, in1=bc(gam[:, HALF:HD], HALF),
-                    op0=ALU.mult, op1=ALU.mult,
-                )
-                nc.vector.tensor_tensor(out=c_t[:], in0=cosv, in1=bc(bet, HD), op=ALU.mult)
-                nc.vector.scalar_tensor_tensor(
-                    out=tmp[:, :, 0:HALF], in0=sinv[:, :, 0:HALF], scalar=-1.0, in1=bc(bet[:, HALF:HD], HALF),
-                    op0=ALU.mult, op1=ALU.mult,
-                )
-                nc.vector.tensor_tensor(
-                    out=tmp[:, :, HALF:HD], in0=sinv[:, :, HALF:HD], in1=bc(bet[:, 0:HALF], HALF), op=ALU.mult
-                )
-                nc.vector.tensor_tensor(out=c_t[:], in0=c_t[:], in1=tmp[:], op=ALU.add)
-                tabs[kind] = (ab_t, c_t)
-                w += 1
-
         wides = {}
         grps = {}
         codes = {}
-        accs = {}
 
         def widen_plane(s, t):
             def run():
@@ -200,17 +198,23 @@ def tile_gqa_flashattn_pa_kernel(
             return run
 
         def prep_scalar_ops(s):
-            kind = GROUPS[s // NG][0]
-            if kind == "q":
+            ops = []
+            if GROUPS[s // NG][0] == "q":
                 wides[s] = wide_pool.tile([P, 4, GW], BF16, name="wide", tag="wide")
-                return [widen_plane(s, t) for t in range(4)]
-            grps[s] = grp_pool.tile([P, GW, 4], BF16, name="grp", tag="grp", align_bytes=64)
-            return [scalar_interleave(s, part) for part in range(2)]
+                ops = [widen_plane(s, t) for t in range(4)]
+            elif s in S_INTER:
+                grps[s] = grp_pool.tile([P, GW, 4], BF16, name="grp", tag="grp", align_bytes=64)
+                ops = [scalar_interleave(s, part) for part in range(2)]
+            if 1 <= s <= NT:
+                ops.extend([x_turn(s - 1, half) for half in range(2)])
+            return ops
 
         def interleave(s):
-            if GROUPS[s // NG][0] == "q":
-                grps[s] = grp_pool.tile([P, GW, 4], BF16, name="grp", tag="grp", align_bytes=64)
-                nc.vector.tensor_copy(out=grps[s][:], in_=wides[s][:].rearrange("p t n -> p n t"))
+            if s in S_INTER:
+                return
+            src = wides[s] if GROUPS[s // NG][0] == "q" else raw[s]
+            grps[s] = grp_pool.tile([P, GW, 4], BF16, name="grp", tag="grp", align_bytes=64)
+            nc.vector.tensor_copy(out=grps[s][:], in_=src[:].rearrange("p t n -> p n t"))
 
         def quantize(s):
             wc = code_pool.tile([P, GW], U32, name="wc", tag="wc", align_bytes=64)
@@ -220,17 +224,21 @@ def tile_gqa_flashattn_pa_kernel(
             )
             codes[s] = (wc, ws)
 
-        def multiply(s):
-            c = s // NG
-            g = s % NG
-            if g == 0:
-                for i in range(NT):
-                    accs[(c, i)] = psum.tile([P, GW], F32, name="acc", tag="bank%d" % ((c % 2) * NT + i))
-            wc, ws = codes[s]
-            for i in range(NT):
+        accs = {}
+        stats = {}
+        work = {}
+        rts = {}
+        sums = {}
+
+        def unit_matmuls(e):
+            c = e // NT
+            i = e % NT
+            acc = psum.tile([P, GW], F32, name="acc", tag="b%d" % (e % 4 + (4 if e >= NNORM else 0)))
+            for g in range(NG):
+                wc, ws = codes[NG * c + g]
                 lo = (NG * i + g) * P
                 nc.tensor.matmul_mx(
-                    out=accs[(c, i)][:],
+                    out=acc[:],
                     lhsT=xc[:, lo : lo + P].bitcast(FP8X4),
                     lhsT_scale=xs[:, lo : lo + P],
                     rhs=wc[:].bitcast(FP8X4),
@@ -238,126 +246,140 @@ def tile_gqa_flashattn_pa_kernel(
                     start=(g == 0),
                     stop=(g == NG - 1),
                 )
+            accs[e] = acc
 
-        stats = {}
-        work = {}
+        def head_sum(e, h):
+            def run():
+                junk = junk_pool.tile([P, HD], BF16, name="junk", tag="junk")
+                nc.scalar.activation(
+                    out=junk[:], in_=accs[e][:, h * HD : (h + 1) * HD], func=ACT.Identity,
+                    accum_out=stats[e][:, h : h + 1],
+                )
+            return run
 
-        def stats_segments(e):
-            c = e // NT
-            i = e % NT
-            acc = accs[(c, i)]
-            st = stat_pool.tile([P, 16], F32, name="st", tag="st")
-            stats[e] = st
+        def neg_mean(e):
+            def run():
+                nc.scalar.activation(out=stats[e][:, 4:8], in_=stats[e][:, 0:4], func=ACT.Copy, scale=-1.0 / HD)
+            return run
 
-            def head_sum(h):
-                def run():
-                    junk = junk_pool.tile([P, HD], BF16, name="junk", tag="junk")
-                    nc.scalar.activation(
-                        out=junk[:], in_=acc[:, h * HD : (h + 1) * HD], func=ACT.Identity, accum_out=st[:, h : h + 1]
-                    )
-                return run
+        def head_sq(e, h):
+            def run():
+                junk = junk_pool.tile([P, HD], BF16, name="junk", tag="junk")
+                nc.scalar.activation(
+                    out=junk[:], in_=accs[e][:, h * HD : (h + 1) * HD], func=ACT.Square,
+                    bias=stats[e][:, 4 + h : 5 + h], accum_out=stats[e][:, 8 + h : 9 + h],
+                )
+            return run
 
-            def neg_mean():
-                nc.scalar.activation(out=st[:, 4:8], in_=st[:, 0:4], func=ACT.Copy, scale=-1.0 / HD)
+        def std_dev(e):
+            def run():
+                nc.scalar.activation(
+                    out=stats[e][:, 12:16], in_=stats[e][:, 8:12], func=ACT.Sqrt, scale=1.0 / HD, bias=EPS
+                )
+            return run
 
-            def head_sq(h):
-                def run():
-                    junk = junk_pool.tile([P, HD], BF16, name="junk", tag="junk")
-                    nc.scalar.activation(
-                        out=junk[:], in_=acc[:, h * HD : (h + 1) * HD], func=ACT.Square,
-                        bias=st[:, 4 + h : 5 + h], accum_out=st[:, 8 + h : 9 + h],
-                    )
-                return run
-
-            def std():
-                nc.scalar.activation(out=st[:, 12:16], in_=st[:, 8:12], func=ACT.Sqrt, scale=1.0 / HD, bias=EPS)
-
-            return [[head_sum(h) for h in range(4)], [neg_mean], [head_sq(h) for h in range(4)], [std]]
+        def recip(e):
+            rt = stat_pool.tile([P, 4], F32, name="rt", tag="rt")
+            nc.vector.reciprocal(out=rt[:], in_=stats[e][:, 12:16])
+            rts[e] = rt
 
         def epi_ab(e):
-            c = e // NT
+            kind = GROUPS[e // NT][0]
             i = e % NT
-            kind = GROUPS[c][0]
-            acc = accs[(c, i)]
-            st = stats[e]
-            rt = stat_pool.tile([P, 4], F32, name="rt", tag="rt")
-            nc.vector.reciprocal(out=rt[:], in_=st[:, 12:16])
             ab = ab_pool.tile([P, 4, 2, HD], F32, name="ab", tag="ab")
             for h in range(4):
                 nc.vector.scalar_tensor_tensor(
                     out=ab[:, h, :, :],
-                    in0=acc[:, h * HD : (h + 1) * HD].unsqueeze(1).to_broadcast([P, 2, HD]),
-                    scalar=st[:, 4 + h : 5 + h],
+                    in0=accs[e][:, h * HD : (h + 1) * HD].unsqueeze(1).to_broadcast([P, 2, HD]),
+                    scalar=stats[e][:, 4 + h : 5 + h],
                     in1=tabs[kind][0][:, i, :, :],
                     op0=ALU.add,
                     op1=ALU.mult,
                 )
-            work[e] = (ab, rt)
+            work[e] = ab
 
-        def out_view(c, i):
-            kind, idx = GROUPS[c]
+        def tensor_add(e):
+            ab = work[e]
+            cps = psum.tile([P, 4, HD], F32, name="cps", tag="b%d" % (4 + e % 4))
+            nc.tensor.matmul(out=cps[:], lhsT=ident[:], rhs=ab[:, :, 1, :], start=True, stop=False)
+            nc.tensor.matmul(out=cps[:, :, 0:HALF], lhsT=ident[:], rhs=ab[:, :, 0, HALF:HD], start=False, stop=False)
+            nc.tensor.matmul(out=cps[:, :, HALF:HD], lhsT=ident[:], rhs=ab[:, :, 0, 0:HALF], start=False, stop=True)
+            sums[e] = cps
+
+        def vector_add(e):
+            ab = work[e]
+            cc = c_pool.tile([P, 4, HD], F32, name="cc", tag="cc")
+            nc.vector.tensor_tensor(out=cc[:, :, 0:HALF], in0=ab[:, :, 1, 0:HALF], in1=ab[:, :, 0, HALF:HD], op=ALU.add)
+            nc.vector.tensor_tensor(out=cc[:, :, HALF:HD], in0=ab[:, :, 1, HALF:HD], in1=ab[:, :, 0, 0:HALF], op=ALU.add)
+            sums[e] = cc
+
+        def out_view(e):
+            kind, idx = GROUPS[e // NT]
+            i = e % NT
             dram = out_q if kind == "q" else (out_k if kind == "k" else out_v)
             return dram[0, 4 * idx : 4 * idx + 4, i * P : (i + 1) * P, :].rearrange("h p d -> p h d")
 
-        def epi_rest(e):
-            c = e // NT
+        def final(e):
+            kind = GROUPS[e // NT][0]
             i = e % NT
-            kind = GROUPS[c][0]
-            ab, rt = work[e]
-            cc = c_pool.tile([P, 4, HD], F32, name="cc", tag="cc")
-            nc.vector.tensor_tensor(out=cc[:, :, 0:HALF], in0=ab[:, :, 0, 0:HALF], in1=ab[:, :, 1, HALF:HD], op=ALU.add)
-            nc.vector.tensor_tensor(out=cc[:, :, HALF:HD], in0=ab[:, :, 0, HALF:HD], in1=ab[:, :, 1, 0:HALF], op=ALU.add)
             o = o_pool.tile([P, 4, HD], F32, name="o", tag="o")
             for h in range(4):
                 nc.vector.scalar_tensor_tensor(
-                    out=o[:, h, :], in0=cc[:, h, :], scalar=rt[:, h : h + 1], in1=tabs[kind][1][:, i, :],
+                    out=o[:, h, :], in0=sums[e][:, h, :], scalar=rts[e][:, h : h + 1], in1=tabs[kind][1][:, i, :],
                     op0=ALU.mult, op1=ALU.add,
                 )
-            nc.sync.dma_start(out=out_view(c, i), in_=o[:])
+            nc.sync.dma_start(out=out_view(e), in_=o[:])
 
-        def copy_values(c):
-            for i in range(NT):
-                o = o_pool.tile([P, 4, HD], F32, name="o", tag="o")
-                flat = o[:].rearrange("p h d -> p (h d)")
-                if i % 2 == 0:
-                    nc.scalar.copy(out=flat, in_=accs[(c, i)][:])
-                else:
-                    nc.vector.tensor_copy(out=flat, in_=accs[(c, i)][:])
-                nc.sync.dma_start(out=out_view(c, i), in_=o[:])
+        def copy_values(e):
+            o = o_pool.tile([P, 4, HD], F32, name="o", tag="o")
+            nc.scalar.copy(out=o[:].rearrange("p h d -> p (h d)"), in_=accs[e][:])
+            nc.sync.dma_start(out=out_view(e), in_=o[:])
 
         def normed(e):
-            return 0 <= e < NCHUNK and GROUPS[e // NT][0] != "v"
+            return 0 <= e < NNORM
 
-        for s in range(NCHUNK + DV + 1):
-            fill = prep_scalar_ops(s) if s < NCHUNK else []
-            segs = stats_segments(s - DS) if normed(s - DS) else [[], [], [], []]
-            for op in weave(segs, fill):
+        for s in range(-SA, NCHUNK + 4):
+            if normed(s - 5):
+                unit_matmuls(s - 5)
+                stats[s - 5] = stat_pool.tile([P, 16], F32, name="st", tag="st")
+            if s == NCHUNK + 1:
+                for e in range(NNORM, NCHUNK):
+                    unit_matmuls(e)
+            fill = prep_scalar_ops(s + SA) if s + SA < NCHUNK else []
+            seq = list(fill[0:1])
+            if normed(s - 6):
+                seq.append(std_dev(s - 6))
+            seq.extend(fill[1:2])
+            if normed(s - 5):
+                seq.extend([head_sum(s - 5, h) for h in range(4)])
+                seq.extend(fill[2:3])
+                seq.append(neg_mean(s - 5))
+                seq.extend(fill[3:4])
+                seq.extend([head_sq(s - 5, h) for h in range(4)])
+                seq.extend(fill[4:])
+            else:
+                seq.extend(fill[2:])
+            for op in seq:
                 op()
+            if s == NCHUNK + 1:
+                for e in range(NNORM, NCHUNK):
+                    copy_values(e)
             if s == 0:
-                x_turn(0)
-                x_turn(1)
-            if s == 1:
-                x_turn(2)
-                x_turn(3)
+                build_tables("q")
+                build_tables("k")
+            if normed(s - 7):
+                recip(s - 7)
+                if s - 7 >= PE_ADD:
+                    vector_add(s - 7)
             if 1 <= s <= NCHUNK:
                 interleave(s - 1)
-            if s == 1:
-                x_quant(0)
-                x_quant(1)
-            if s == 2:
-                x_quant(2)
-                x_quant(3)
-            if s == 4:
-                build_tables()
-            if normed(s - DV):
-                epi_ab(s - DV)
+            if 1 <= s <= NT:
+                x_quant(s - 1)
+            if normed(s - 6):
+                epi_ab(s - 6)
+                if s - 6 < PE_ADD:
+                    tensor_add(s - 6)
+            if normed(s - 7):
+                final(s - 7)
             if 1 <= s <= NCHUNK:
                 quantize(s - 1)
-            if s == 2:
-                multiply(0)
-            if 2 <= s <= NCHUNK:
-                multiply(s - 1)
-            if normed(s - DV):
-                epi_rest(s - DV)
-            if s >= 5 and (s - 5) % NG == 0 and (s - 5) // NG < len(GROUPS) and GROUPS[(s - 5) // NG][0] == "v":
-                copy_values((s - 5) // NG)

@@ -194,7 +194,10 @@ def tile_gqa_flashattn_pa_kernel(
             def run():
                 lo = part * (GW // 2)
                 hi = lo + GW // 2
-                nc.scalar.copy(out=grps[s][:, lo:hi, :], in_=raw[s][:, :, lo:hi].rearrange("p t n -> p n t"))
+                nc.scalar.copy(
+                    out=grps[s][:, lo:hi, :].rearrange("p (c i) t -> p c t i", i=4),
+                    in_=raw[s][:, :, lo:hi].rearrange("p t (c i) -> p c t i", i=4),
+                )
             return run
 
         def prep_scalar_ops(s):
@@ -214,7 +217,9 @@ def tile_gqa_flashattn_pa_kernel(
                 return
             src = wides[s] if GROUPS[s // NG][0] == "q" else raw[s]
             grps[s] = grp_pool.tile([P, GW, 4], BF16, name="grp", tag="grp", align_bytes=64)
-            nc.vector.tensor_copy(out=grps[s][:], in_=src[:].rearrange("p t n -> p n t"))
+            nc.vector.tensor_copy(
+                out=grps[s][:].rearrange("p (c i) t -> p c t i", i=4), in_=src[:].rearrange("p t (c i) -> p c t i", i=4)
+            )
 
         def quantize(s):
             wc = code_pool.tile([P, GW], U32, name="wc", tag="wc", align_bytes=64)

@@ -25,7 +25,7 @@ GROUPS = (("q", 0), ("q", 1), ("q", 2), ("q", 3), ("k", 0), ("v", 0))
 NCHUNK = 24
 NNORM = 20
 SA = 2
-S_INTER = (20, 21, 22, 23)
+S_INTER = (21, 22, 23)
 PE_ADD = 18
 
 
@@ -53,7 +53,7 @@ def tile_gqa_flashattn_pa_kernel(
         one = const.tile([P, 1], F32, name="one", tag="one")
         nc.gpsimd.memset(one[:], 1.0)
         warm = const.tile([P, 1], F32, name="warm", tag="warm")
-        nc.scalar.activation(out=warm[:], in_=one[:], func=ACT.Sqrt)
+        nc.scalar.activation(out=warm[:], in_=one[:], func=ACT.Abs_reciprocal_sqrt)
         rmat = const.tile([P, 4, P], BF16, name="rmat", tag="rmat")
         make_identity(nc, rmat[:, 1, :])
         nc.gpsimd.tensor_copy(out=rmat[:, 2, :], in_=rmat[:, 1, :])
@@ -192,8 +192,8 @@ def tile_gqa_flashattn_pa_kernel(
 
         def scalar_interleave(s, part):
             def run():
-                lo = part * (GW // 2)
-                hi = lo + GW // 2
+                lo = part * GW
+                hi = lo + GW
                 nc.scalar.copy(
                     out=grps[s][:, lo:hi, :].rearrange("p (c i) t -> p c t i", i=4),
                     in_=raw[s][:, :, lo:hi].rearrange("p t (c i) -> p c t i", i=4),
@@ -207,7 +207,7 @@ def tile_gqa_flashattn_pa_kernel(
                 ops = [widen_plane(s, t) for t in range(4)]
             elif s in S_INTER:
                 grps[s] = grp_pool.tile([P, GW, 4], BF16, name="grp", tag="grp", align_bytes=64)
-                ops = [scalar_interleave(s, part) for part in range(2)]
+                ops = [scalar_interleave(s, 0)]
             if 1 <= s <= NT:
                 ops.extend([x_turn(s - 1, half) for half in range(2)])
             return ops
@@ -232,7 +232,6 @@ def tile_gqa_flashattn_pa_kernel(
         accs = {}
         stats = {}
         work = {}
-        rts = {}
         sums = {}
 
         def unit_matmuls(e):
@@ -257,14 +256,9 @@ def tile_gqa_flashattn_pa_kernel(
             def run():
                 junk = junk_pool.tile([P, HD], BF16, name="junk", tag="junk")
                 nc.scalar.activation(
-                    out=junk[:], in_=accs[e][:, h * HD : (h + 1) * HD], func=ACT.Identity,
-                    accum_out=stats[e][:, h : h + 1],
+                    out=junk[:], in_=accs[e][:, h * HD : (h + 1) * HD], func=ACT.Identity, scale=-1.0 / HD,
+                    accum_out=stats[e][:, 4 + h : 5 + h],
                 )
-            return run
-
-        def neg_mean(e):
-            def run():
-                nc.scalar.activation(out=stats[e][:, 4:8], in_=stats[e][:, 0:4], func=ACT.Copy, scale=-1.0 / HD)
             return run
 
         def head_sq(e, h):
@@ -279,14 +273,9 @@ def tile_gqa_flashattn_pa_kernel(
         def std_dev(e):
             def run():
                 nc.scalar.activation(
-                    out=stats[e][:, 12:16], in_=stats[e][:, 8:12], func=ACT.Sqrt, scale=1.0 / HD, bias=EPS
+                    out=stats[e][:, 12:16], in_=stats[e][:, 8:12], func=ACT.Abs_reciprocal_sqrt, scale=1.0 / HD, bias=EPS
                 )
             return run
-
-        def recip(e):
-            rt = stat_pool.tile([P, 4], F32, name="rt", tag="rt")
-            nc.vector.reciprocal(out=rt[:], in_=stats[e][:, 12:16])
-            rts[e] = rt
 
         def epi_ab(e):
             kind = GROUPS[e // NT][0]
@@ -330,7 +319,7 @@ def tile_gqa_flashattn_pa_kernel(
             o = o_pool.tile([P, 4, HD], F32, name="o", tag="o")
             for h in range(4):
                 nc.vector.scalar_tensor_tensor(
-                    out=o[:, h, :], in0=sums[e][:, h, :], scalar=rts[e][:, h : h + 1], in1=tabs[kind][1][:, i, :],
+                    out=o[:, h, :], in0=sums[e][:, h, :], scalar=stats[e][:, 12 + h : 13 + h], in1=tabs[kind][1][:, i, :],
                     op0=ALU.mult, op1=ALU.add,
                 )
             nc.sync.dma_start(out=out_view(e), in_=o[:])
@@ -357,9 +346,7 @@ def tile_gqa_flashattn_pa_kernel(
             seq.extend(fill[1:2])
             if normed(s - 5):
                 seq.extend([head_sum(s - 5, h) for h in range(4)])
-                seq.extend(fill[2:3])
-                seq.append(neg_mean(s - 5))
-                seq.extend(fill[3:4])
+                seq.extend(fill[2:4])
                 seq.extend([head_sq(s - 5, h) for h in range(4)])
                 seq.extend(fill[4:])
             else:
@@ -372,10 +359,8 @@ def tile_gqa_flashattn_pa_kernel(
             if s == 0:
                 build_tables("q")
                 build_tables("k")
-            if normed(s - 7):
-                recip(s - 7)
-                if s - 7 >= PE_ADD:
-                    vector_add(s - 7)
+            if normed(s - 7) and s - 7 >= PE_ADD:
+                vector_add(s - 7)
             if 1 <= s <= NCHUNK:
                 interleave(s - 1)
             if 1 <= s <= NT:

@@ -26,7 +26,18 @@ NCHUNK = 24
 NNORM = 20
 SA = 2
 S_INTER = (21, 22, 23)
-PE_ADD = 18
+V_ADD = (18, 19)
+HEAD_CHUNKS = 4
+V_EVERY = 0
+VW = 1
+
+
+def v_planes(s):
+    if s >= 16:
+        return ()
+    if s < HEAD_CHUNKS:
+        return (2, 3)
+    return (3,) if V_EVERY and s % V_EVERY == 0 else ()
 
 
 def tile_gqa_flashattn_pa_kernel(
@@ -46,7 +57,7 @@ def tile_gqa_flashattn_pa_kernel(
         junk_pool = ctx.enter_context(tc.tile_pool(name="junk", bufs=4))
         ab_pool = ctx.enter_context(tc.tile_pool(name="ab", bufs=3))
         c_pool = ctx.enter_context(tc.tile_pool(name="cc", bufs=2))
-        o_pool = ctx.enter_context(tc.tile_pool(name="o", bufs=4))
+        o_pool = ctx.enter_context(tc.tile_pool(name="o", bufs=8))
         psum = ctx.enter_context(tc.psum_pool(name="psum", bufs=1))
         ctx.enter_context(tc.manual_schedule())
 
@@ -204,13 +215,21 @@ def tile_gqa_flashattn_pa_kernel(
             ops = []
             if GROUPS[s // NG][0] == "q":
                 wides[s] = wide_pool.tile([P, 4, GW], BF16, name="wide", tag="wide")
-                ops = [widen_plane(s, t) for t in range(4)]
+                ops = [widen_plane(s, t) for t in range(4) if t not in v_planes(s)]
             elif s in S_INTER:
                 grps[s] = grp_pool.tile([P, GW, 4], BF16, name="grp", tag="grp", align_bytes=64)
                 ops = [scalar_interleave(s, 0)]
             if 1 <= s <= NT:
                 ops.extend([x_turn(s - 1, half) for half in range(2)])
             return ops
+
+        def vector_widen(s):
+            g = s % NG
+            for t in v_planes(s):
+                nc.vector.tensor_scalar(
+                    out=wides[s][:, t, :], in0=raw[s][:, t, :].bitcast(FP8), scalar1=wsc[:, 4 * g + t : 4 * g + t + 1],
+                    scalar2=None, op0=ALU.mult,
+                )
 
         def interleave(s):
             if s in S_INTER:
@@ -359,7 +378,9 @@ def tile_gqa_flashattn_pa_kernel(
             if s == 0:
                 build_tables("q")
                 build_tables("k")
-            if normed(s - 7) and s - 7 >= PE_ADD:
+            if 0 <= s + VW < NCHUNK:
+                vector_widen(s + VW)
+            if normed(s - 7) and s - 7 in V_ADD:
                 vector_add(s - 7)
             if 1 <= s <= NCHUNK:
                 interleave(s - 1)
@@ -367,7 +388,7 @@ def tile_gqa_flashattn_pa_kernel(
                 x_quant(s - 1)
             if normed(s - 6):
                 epi_ab(s - 6)
-                if s - 6 < PE_ADD:
+                if s - 6 not in V_ADD:
                     tensor_add(s - 6)
             if normed(s - 7):
                 final(s - 7)

@@ -25,8 +25,8 @@ GROUPS = (("q", 0), ("q", 1), ("q", 2), ("q", 3), ("k", 0), ("v", 0))
 NCHUNK = 24
 NNORM = 20
 SA = 2
-S_INTER = (21, 22, 23)
-V_ADD = (18, 19)
+S_INTER = (17, 18, 20, 21, 23)
+V_ADD = (14, 17, 18, 19)
 HEAD_CHUNKS = 4
 V_EVERY = 0
 VW = 1
@@ -271,6 +271,28 @@ def tile_gqa_flashattn_pa_kernel(
                 )
             accs[e] = acc
 
+        def value_start_step(e):
+            users = [n for n in range(NNORM) if n % 4 == e % 4 and n not in V_ADD]
+            return max(users) + 8
+
+        def value_passes(e, g_lo, g_hi):
+            c = e // NT
+            i = e % NT
+            if e not in accs:
+                accs[e] = psum.tile([P, GW], F32, name="acc", tag="b%d" % (4 + e % 4))
+            for g in range(g_lo, g_hi):
+                wc, ws = codes[NG * c + g]
+                lo = (NG * i + g) * P
+                nc.tensor.matmul_mx(
+                    out=accs[e][:],
+                    lhsT=xc[:, lo : lo + P].bitcast(FP8X4),
+                    lhsT_scale=xs[:, lo : lo + P],
+                    rhs=wc[:].bitcast(FP8X4),
+                    rhs_scale=ws[:],
+                    start=(g == 0),
+                    stop=(g == NG - 1),
+                )
+
         def head_sum(e, h):
             def run():
                 junk = junk_pool.tile([P, HD], BF16, name="junk", tag="junk")
@@ -351,13 +373,16 @@ def tile_gqa_flashattn_pa_kernel(
         def normed(e):
             return 0 <= e < NNORM
 
+        done = {e: 0 for e in range(NNORM, NCHUNK)}
         for s in range(-SA, NCHUNK + 4):
             if normed(s - 5):
                 unit_matmuls(s - 5)
                 stats[s - 5] = stat_pool.tile([P, 16], F32, name="st", tag="st")
-            if s == NCHUNK + 1:
-                for e in range(NNORM, NCHUNK):
-                    unit_matmuls(e)
+            for e in range(NNORM, NCHUNK):
+                ready = min(NG, s - (NNORM + 1))
+                if s >= value_start_step(e) and ready > done[e]:
+                    value_passes(e, done[e], ready)
+                    done[e] = ready
             fill = prep_scalar_ops(s + SA) if s + SA < NCHUNK else []
             seq = list(fill[0:1])
             if normed(s - 6):

@@ -30,6 +30,11 @@ V_ADD = (14, 17, 18, 19)
 HEAD_CHUNKS = 4
 V_EVERY = 0
 VW = 1
+L_MX = 5
+L_ST = 5
+L_AB = 7
+L_ADD = 8
+L_FIN = 9
 
 
 def v_planes(s):
@@ -53,7 +58,7 @@ def tile_gqa_flashattn_pa_kernel(
         wide_pool = ctx.enter_context(tc.tile_pool(name="wide", bufs=6))
         grp_pool = ctx.enter_context(tc.tile_pool(name="grp", bufs=5))
         code_pool = ctx.enter_context(tc.tile_pool(name="codes", bufs=10))
-        stat_pool = ctx.enter_context(tc.tile_pool(name="stats", bufs=4))
+        stat_pool = ctx.enter_context(tc.tile_pool(name="stats", bufs=6))
         junk_pool = ctx.enter_context(tc.tile_pool(name="junk", bufs=4))
         ab_pool = ctx.enter_context(tc.tile_pool(name="ab", bufs=3))
         c_pool = ctx.enter_context(tc.tile_pool(name="cc", bufs=2))
@@ -273,7 +278,7 @@ def tile_gqa_flashattn_pa_kernel(
 
         def value_start_step(e):
             users = [n for n in range(NNORM) if n % 4 == e % 4 and n not in V_ADD]
-            return max(users) + 8
+            return max(users) + L_FIN + 1
 
         def value_passes(e, g_lo, g_hi):
             c = e // NT
@@ -374,48 +379,54 @@ def tile_gqa_flashattn_pa_kernel(
             return 0 <= e < NNORM
 
         done = {e: 0 for e in range(NNORM, NCHUNK)}
-        for s in range(-SA, NCHUNK + 4):
-            if normed(s - 5):
-                unit_matmuls(s - 5)
-                stats[s - 5] = stat_pool.tile([P, 16], F32, name="st", tag="st")
+        full = []
+        for s in range(-SA, NCHUNK + L_FIN + 2):
+            if normed(s - L_MX):
+                unit_matmuls(s - L_MX)
+            if normed(s - L_ADD) and s - L_ADD not in V_ADD:
+                tensor_add(s - L_ADD)
             for e in range(NNORM, NCHUNK):
                 ready = min(NG, s - (NNORM + 1))
                 if s >= value_start_step(e) and ready > done[e]:
                     value_passes(e, done[e], ready)
                     done[e] = ready
+                    if ready == NG:
+                        full.append(e)
+            if normed(s - L_ST):
+                stats[s - L_ST] = stat_pool.tile([P, 16], F32, name="st", tag="st")
             fill = prep_scalar_ops(s + SA) if s + SA < NCHUNK else []
             seq = list(fill[0:1])
-            if normed(s - 6):
-                seq.append(std_dev(s - 6))
+            if normed(s - L_ST - 1):
+                seq.append(std_dev(s - L_ST - 1))
             seq.extend(fill[1:2])
-            if normed(s - 5):
-                seq.extend([head_sum(s - 5, h) for h in range(4)])
+            if normed(s - L_ST):
+                seq.extend([head_sum(s - L_ST, h) for h in range(4)])
                 seq.extend(fill[2:4])
-                seq.extend([head_sq(s - 5, h) for h in range(4)])
+                seq.extend([head_sq(s - L_ST, h) for h in range(4)])
                 seq.extend(fill[4:])
             else:
                 seq.extend(fill[2:])
             for op in seq:
                 op()
-            if s == NCHUNK + 1:
-                for e in range(NNORM, NCHUNK):
-                    copy_values(e)
+            for e in full:
+                copy_values(e)
+            full.clear()
             if s == 0:
                 build_tables("q")
                 build_tables("k")
             if 0 <= s + VW < NCHUNK:
                 vector_widen(s + VW)
-            if normed(s - 7) and s - 7 in V_ADD:
-                vector_add(s - 7)
+            if normed(s - L_AB - 1) and s - L_AB - 1 in V_ADD:
+                vector_add(s - L_AB - 1)
             if 1 <= s <= NCHUNK:
                 interleave(s - 1)
             if 1 <= s <= NT:
                 x_quant(s - 1)
-            if normed(s - 6):
-                epi_ab(s - 6)
-                if s - 6 not in V_ADD:
-                    tensor_add(s - 6)
-            if normed(s - 7):
-                final(s - 7)
+            if normed(s - L_AB):
+                epi_ab(s - L_AB)
+            if normed(s - L_AB - 1) and s - L_AB - 1 in V_ADD:
+                final(s - L_AB - 1)
+            if normed(s - L_FIN) and s - L_FIN not in V_ADD:
+                final(s - L_FIN)
             if 1 <= s <= NCHUNK:
                 quantize(s - 1)

@@ -30,6 +30,8 @@ V_ADD = (14, 17, 18, 19)
 HEAD_CHUNKS = 4
 V_EVERY = 0
 VW = 1
+Q_TABLES_AT = 0
+K_TABLES_AT = 8
 L_MX = 5
 L_ST = 5
 L_AB = 7
@@ -173,7 +175,7 @@ def tile_gqa_flashattn_pa_kernel(
         def x_turn(i, half):
             def run():
                 words = xr[i][:].bitcast(F32)
-                xt = psum.tile([P, 2, 2, P], F32, name="xt", tag="b%d" % (2 * i + half))
+                xt = psum.tile([P, 2, 2, P], F32, name="xt", tag="b%d" % ((2 * i + half) % 6))
                 for gl in range(2):
                     g = 2 * half + gl
                     for u in range(2):
@@ -411,8 +413,9 @@ def tile_gqa_flashattn_pa_kernel(
             for e in full:
                 copy_values(e)
             full.clear()
-            if s == 0:
+            if s == Q_TABLES_AT:
                 build_tables("q")
+            if s == K_TABLES_AT:
                 build_tables("k")
             if 0 <= s + VW < NCHUNK:
                 vector_widen(s + VW)

@@ -26,10 +26,11 @@ NCHUNK = 24
 NNORM = 20
 SA = 2
 S_INTER = (17, 18, 20, 21, 23)
-V_ADD = (14, 17, 18, 19)
+V_ADD = (10, 13, 16, 17, 18, 19)
 HEAD_CHUNKS = 4
 V_EVERY = 0
 VW = 1
+X_LATE = 1
 Q_TABLES_AT = 0
 K_TABLES_AT = 8
 L_MX = 5
@@ -226,8 +227,8 @@ def tile_gqa_flashattn_pa_kernel(
             elif s in S_INTER:
                 grps[s] = grp_pool.tile([P, GW, 4], BF16, name="grp", tag="grp", align_bytes=64)
                 ops = [scalar_interleave(s, 0)]
-            if 1 <= s <= NT:
-                ops.extend([x_turn(s - 1, half) for half in range(2)])
+            if 1 + X_LATE <= s <= NT + X_LATE:
+                ops.extend([x_turn(s - 1 - X_LATE, half) for half in range(2)])
             return ops
 
         def vector_widen(s):
@@ -423,8 +424,8 @@ def tile_gqa_flashattn_pa_kernel(
                 vector_add(s - L_AB - 1)
             if 1 <= s <= NCHUNK:
                 interleave(s - 1)
-            if 1 <= s <= NT:
-                x_quant(s - 1)
+            if 1 + X_LATE <= s <= NT + X_LATE:
+                x_quant(s - 1 - X_LATE)
             if normed(s - L_AB):
                 epi_ab(s - L_AB)
             if normed(s - L_AB - 1) and s - L_AB - 1 in V_ADD:

@@ -330,7 +330,7 @@ def tile_gqa_flashattn_pa_kernel(
             kind = GROUPS[e // NT][0]
             i = e % NT
             ab = ab_pool.tile([P, 4, 2, HD], F32, name="ab", tag="ab")
-            for h in range(4):
+            for h in (3, 2, 1, 0):
                 nc.vector.scalar_tensor_tensor(
                     out=ab[:, h, :, :],
                     in0=accs[e][:, h * HD : (h + 1) * HD].unsqueeze(1).to_broadcast([P, 2, HD]),
@@ -345,15 +345,21 @@ def tile_gqa_flashattn_pa_kernel(
             ab = work[e]
             cps = psum.tile([P, 4, HD], F32, name="cps", tag="b%d" % (4 + e % 4))
             nc.tensor.matmul(out=cps[:], lhsT=ident[:], rhs=ab[:, :, 1, :], start=True, stop=False)
-            nc.tensor.matmul(out=cps[:, :, 0:HALF], lhsT=ident[:], rhs=ab[:, :, 0, HALF:HD], start=False, stop=False)
-            nc.tensor.matmul(out=cps[:, :, HALF:HD], lhsT=ident[:], rhs=ab[:, :, 0, 0:HALF], start=False, stop=True)
+            nc.tensor.matmul(
+                out=cps[:].rearrange("p h (a d) -> p h a d", a=2), lhsT=ident[:],
+                rhs=ab[:, :, 0, :].rearrange("p h (a d) -> p h a d", a=2)[:, :, ::-1, :], start=False, stop=True,
+            )
             sums[e] = cps
 
         def vector_add(e):
             ab = work[e]
             cc = c_pool.tile([P, 4, HD], F32, name="cc", tag="cc")
-            nc.vector.tensor_tensor(out=cc[:, :, 0:HALF], in0=ab[:, :, 1, 0:HALF], in1=ab[:, :, 0, HALF:HD], op=ALU.add)
-            nc.vector.tensor_tensor(out=cc[:, :, HALF:HD], in0=ab[:, :, 1, HALF:HD], in1=ab[:, :, 0, 0:HALF], op=ALU.add)
+            nc.vector.tensor_tensor(
+                out=cc[:].rearrange("p h (a d) -> p h a d", a=2),
+                in0=ab[:, :, 1, :].rearrange("p h (a d) -> p h a d", a=2),
+                in1=ab[:, :, 0, :].rearrange("p h (a d) -> p h a d", a=2)[:, :, ::-1, :],
+                op=ALU.add,
+            )
             sums[e] = cc
 
         def out_view(e):

@@ -25,27 +25,30 @@ GROUPS = (("q", 0), ("q", 1), ("q", 2), ("q", 3), ("k", 0), ("v", 0))
 NCHUNK = 24
 NNORM = 20
 SA = 2
-S_INTER = (17, 18, 20, 21, 23)
-V_ADD = (10, 13, 16, 17, 18, 19)
+S_INTER = (12, 15, 17, 18, 20, 21, 23, )
+V_ADD = (13, 16, 17, 18, 19, )
+G_INTER = ()
+G_ADD = ()
+S_STAT = (1, 2, 3, 5, 6, 7, 9, 10, 11, 12, 13, 14, 15, 16, 17, 18, 19, )
+G_PIECES = 4
 HEAD_CHUNKS = 4
 V_EVERY = 0
 VW = 1
 X_LATE = 1
-Q_TABLES_AT = 0
-K_TABLES_AT = 8
+MIX_AT = 0
+TABLE_MM = (3, 4, 5, 6)
+TABLE_COPY = (3, 4, 5, 6)
 L_MX = 5
 L_ST = 5
 L_AB = 7
 L_ADD = 8
-L_FIN = 9
+L_FIN = 10
 
 
 def v_planes(s):
     if s >= 16:
         return ()
-    if s < HEAD_CHUNKS:
-        return (2, 3)
-    return (3,) if V_EVERY and s % V_EVERY == 0 else ()
+    return (2, 3) if s < 4 else ((3,) if s < 8 else ())
 
 
 def tile_gqa_flashattn_pa_kernel(
@@ -63,8 +66,9 @@ def tile_gqa_flashattn_pa_kernel(
         code_pool = ctx.enter_context(tc.tile_pool(name="codes", bufs=10))
         stat_pool = ctx.enter_context(tc.tile_pool(name="stats", bufs=6))
         junk_pool = ctx.enter_context(tc.tile_pool(name="junk", bufs=4))
+        inv_pool = ctx.enter_context(tc.tile_pool(name="inv", bufs=6))
         ab_pool = ctx.enter_context(tc.tile_pool(name="ab", bufs=3))
-        c_pool = ctx.enter_context(tc.tile_pool(name="cc", bufs=2))
+        c_pool = ctx.enter_context(tc.tile_pool(name="cc", bufs=4))
         o_pool = ctx.enter_context(tc.tile_pool(name="o", bufs=8))
         psum = ctx.enter_context(tc.psum_pool(name="psum", bufs=1))
         ctx.enter_context(tc.manual_schedule())
@@ -73,17 +77,14 @@ def tile_gqa_flashattn_pa_kernel(
         nc.gpsimd.memset(one[:], 1.0)
         warm = const.tile([P, 1], F32, name="warm", tag="warm")
         nc.scalar.activation(out=warm[:], in_=one[:], func=ACT.Abs_reciprocal_sqrt)
-        rmat = const.tile([P, 4, P], BF16, name="rmat", tag="rmat")
-        make_identity(nc, rmat[:, 1, :])
-        nc.gpsimd.tensor_copy(out=rmat[:, 2, :], in_=rmat[:, 1, :])
-        nc.gpsimd.tensor_copy(out=rmat[:, 0, 0:HALF], in_=rmat[:, 1, 0:HALF])
+        rmat = const.tile([P, 3, P], BF16, name="rmat", tag="rmat")
+        make_identity(nc, rmat[:, 0, :])
+        nc.gpsimd.tensor_copy(out=rmat[:, 1, 0:HALF], in_=rmat[:, 0, HALF:P])
+        nc.gpsimd.tensor_copy(out=rmat[:, 1, HALF:P], in_=rmat[:, 0, 0:HALF])
         nc.gpsimd.tensor_scalar(
-            out=rmat[:, 0, HALF:P], in0=rmat[:, 1, HALF:P], scalar1=-1.0, scalar2=0.0, op0=ALU.mult, op1=ALU.add
+            out=rmat[:, 2, 0:HALF], in0=rmat[:, 0, HALF:P], scalar1=-1.0, scalar2=0.0, op0=ALU.mult, op1=ALU.add
         )
-        nc.gpsimd.tensor_scalar(
-            out=rmat[:, 3, 0:HALF], in0=rmat[:, 1, HALF:P], scalar1=-1.0, scalar2=0.0, op0=ALU.mult, op1=ALU.add
-        )
-        nc.gpsimd.tensor_copy(out=rmat[:, 3, HALF:P], in_=rmat[:, 1, 0:HALF])
+        nc.gpsimd.tensor_copy(out=rmat[:, 2, HALF:P], in_=rmat[:, 0, 0:HALF])
         ident = const.tile([P, P], F32, name="ident", tag="ident")
         make_identity(nc, ident[:])
 
@@ -118,16 +119,12 @@ def tile_gqa_flashattn_pa_kernel(
         gcol = const.tile([P, 4, 16], BF16, name="gcol", tag="gcol")
         v = 0
         with nc.allow_non_contiguous_dma(reason="four vectors of 128 values, one value to a partition"):
-            for vec in (q_gamma, q_beta, k_gamma, k_beta):
+            for vec in (q_gamma, k_gamma, q_beta, k_beta):
                 nc.sync.dma_start(out=gcol[:, v, 0:1], in_=vec.rearrange("(p o) -> p o", o=1))
                 v += 1
-        cs3 = const.tile([P, NT, 3, HD], BF16, name="cs3", tag="cs3")
-        cos_v = cos.rearrange("(i p) d -> p i d", p=P)
-        sin_v = sin.rearrange("(i p) d -> p i d", p=P)
-        nc.sync.dma_start(out=cs3[:, :, 1, :], in_=cos_v)
-        nc.sync.dma_start(out=cs3[:, :, 2, :], in_=sin_v)
-        nc.sync.dma_start(out=cs3[:, :, 0, 0:HALF], in_=sin_v[:, :, HALF:HD])
-        nc.sync.dma_start(out=cs3[:, :, 0, HALF:HD], in_=sin_v[:, :, 0:HALF])
+        cs = const.tile([P, 2, NT, HD], BF16, name="cs", tag="cs")
+        nc.sync.dma_start(out=cs[:, 0, :, :], in_=cos.rearrange("(i p) d -> p i d", p=P))
+        nc.sync.dma_start(out=cs[:, 1, :, :], in_=sin.rearrange("(i p) d -> p i d", p=P))
         load_chunk(1)
         load_x(0)
         load_chunk(2)
@@ -139,35 +136,54 @@ def tile_gqa_flashattn_pa_kernel(
         for s in range(5, NCHUNK):
             load_chunk(s)
 
-        gps = {}
-        w = 0
-        for kind in ("q", "k"):
-            gp = psum.tile([P, 2, 2 * HD], F32, name="gps", tag="b%d" % (6 + w))
-            for j in range(2):
-                nc.tensor.matmul(
-                    out=gp[:, j, :],
-                    lhsT=gcol[:, 2 * w + j, 0:1].to_broadcast([P, P]),
-                    rhs=rmat[:, 2 * j : 2 * j + 2, :],
-                    start=True,
-                    stop=True,
-                )
-            gps[kind] = gp
-            w += 1
-        tabs = {}
+        ab_t = const.tile([P, NT, 2, 2, HD], F32, name="ab_t", tag="ab_t")
+        c_t = const.tile([P, NT, 2, HD], F32, name="c_t", tag="c_t")
+        mix = const.tile([P, 4, 2, HD], BF16, name="mix", tag="mix")
+        cst = const.tile([P, 2, NT, HD], BF16, name="cst", tag="cst")
+        turned = []
 
-        def build_tables(kind):
-            gp = gps[kind]
+        def turn_cos_sin():
+            for w in range(2):
+                ps = psum.tile([P, NT, P], BF16, name="csp", tag="b%d" % (6 + w))
+                for i in range(NT):
+                    nc.tensor.transpose(ps[:, i, :], cs[:, w, i, :], rmat[:, 0, :])
+                turned.append(ps)
+            swp = psum.tile([P, 4], F32, name="swp", tag="b5")
+            nc.tensor.matmul(out=swp[:], lhsT=rmat[:, 2, :], rhs=gcol[:, :, 0], start=True, stop=True)
+            turned.append(swp)
 
-            def bc(j):
-                return gp[:, j, :].rearrange("p (w d) -> p w d", w=2).unsqueeze(1).to_broadcast([P, NT, 2, HD])
+        def mix_matrices():
+            swp = turned[2]
+            for k in range(2):
+                for j, block, col in (
+                    (1, 0, gcol[:, k, 0:1]), (2, 0, gcol[:, 2 + k, 0:1]), (0, 1, swp[:, k : k + 1]), (3, 0, swp[:, 2 + k : 3 + k])
+                ):
+                    nc.vector.tensor_scalar(
+                        out=mix[:, j, k, :], in0=rmat[:, block, :], scalar1=col, scalar2=None, op0=ALU.mult
+                    )
 
-            ab_t = const.tile([P, NT, 2, HD], F32, name="abt_" + kind, tag="abt_" + kind)
-            c_t = const.tile([P, NT, HD], F32, name="ct_" + kind, tag="ct_" + kind)
-            tmp = const.tile([P, NT, 2, HD], F32, name="tmp", tag="tmp")
-            nc.vector.tensor_tensor(out=ab_t[:], in0=cs3[:, :, 0:2, :], in1=bc(0), op=ALU.mult)
-            nc.vector.tensor_tensor(out=tmp[:], in0=cs3[:, :, 1:3, :], in1=bc(1), op=ALU.mult)
-            nc.vector.tensor_tensor(out=c_t[:], in0=tmp[:, :, 0, :], in1=tmp[:, :, 1, :], op=ALU.add)
-            tabs[kind] = (ab_t, c_t)
+        def copy_cos_sin():
+            for w in range(2):
+                nc.vector.tensor_copy(out=cst[:, w, :, :], in_=turned[w][:])
+
+        tab_ps = {}
+
+        def table_matmuls(i):
+            ab = psum.tile([P, 2, 2, HD], F32, name="tab", tag="b6")
+            c = psum.tile([P, 2, HD], F32, name="tc", tag="b7")
+            nc.tensor.matmul(out=ab[:, 1, :, :], lhsT=cst[:, 0, i, :], rhs=mix[:, 1, :, :], start=True, stop=True)
+            nc.tensor.matmul(out=ab[:, 0, :, :], lhsT=cst[:, 1, i, :], rhs=mix[:, 0, :, :], start=True, stop=True)
+            nc.tensor.matmul(out=c[:], lhsT=cst[:, 0, i, :], rhs=mix[:, 2, :, :], start=True, stop=False)
+            nc.tensor.matmul(out=c[:], lhsT=cst[:, 1, i, :], rhs=mix[:, 3, :, :], start=False, stop=True)
+            tab_ps[i] = (ab, c)
+
+        def table_copies(i):
+            def run_ab():
+                nc.scalar.copy(out=ab_t[:, i, :, :, :].rearrange("p k w d -> p w k d"), in_=tab_ps[i][0][:])
+
+            def run_c():
+                nc.scalar.copy(out=c_t[:, i, :, :], in_=tab_ps[i][1][:])
+            return [run_ab, run_c]
 
         xc = const.tile([P, NT * NG * P], U32, name="xc", tag="xc", align_bytes=64)
         xs = const.tile([P, NT * NG * P], U8, name="xs", tag="xs", align_bytes=64)
@@ -209,24 +225,23 @@ def tile_gqa_flashattn_pa_kernel(
                 )
             return run
 
-        def scalar_interleave(s, part):
+        def scalar_interleave(s):
             def run():
-                lo = part * GW
-                hi = lo + GW
+                src = wides[s] if GROUPS[s // NG][0] == "q" else raw[s]
                 nc.scalar.copy(
-                    out=grps[s][:, lo:hi, :].rearrange("p (c i) t -> p c t i", i=4),
-                    in_=raw[s][:, :, lo:hi].rearrange("p t (c i) -> p c t i", i=4),
+                    out=grps[s][:].rearrange("p (c i) t -> p c t i", i=4),
+                    in_=src[:].rearrange("p t (c i) -> p c t i", i=4),
                 )
             return run
 
         def prep_scalar_ops(s):
             ops = []
-            if GROUPS[s // NG][0] == "q":
+            if s - 1 in S_INTER:
+                grps[s - 1] = grp_pool.tile([P, GW, 4], BF16, name="grp", tag="grp", align_bytes=64)
+                ops.append(scalar_interleave(s - 1))
+            if s < NCHUNK and GROUPS[s // NG][0] == "q":
                 wides[s] = wide_pool.tile([P, 4, GW], BF16, name="wide", tag="wide")
-                ops = [widen_plane(s, t) for t in range(4) if t not in v_planes(s)]
-            elif s in S_INTER:
-                grps[s] = grp_pool.tile([P, GW, 4], BF16, name="grp", tag="grp", align_bytes=64)
-                ops = [scalar_interleave(s, 0)]
+                ops.extend([widen_plane(s, t) for t in range(4) if t not in v_planes(s)])
             if 1 + X_LATE <= s <= NT + X_LATE:
                 ops.extend([x_turn(s - 1 - X_LATE, half) for half in range(2)])
             return ops
@@ -239,8 +254,20 @@ def tile_gqa_flashattn_pa_kernel(
                     scalar2=None, op0=ALU.mult,
                 )
 
+        def gpsimd_interleave(s):
+            if s not in G_INTER:
+                return
+            src = wides[s] if GROUPS[s // NG][0] == "q" else raw[s]
+            grps[s] = grp_pool.tile([P, GW, 4], BF16, name="grp", tag="grp", align_bytes=64)
+            w = GW // G_PIECES
+            for c in range(G_PIECES):
+                nc.gpsimd.tensor_scalar(
+                    out=grps[s][:, c * w : (c + 1) * w, :], in0=src[:, :, c * w : (c + 1) * w].rearrange("p t n -> p n t"),
+                    scalar1=1.0, scalar2=0.0, op0=ALU.mult, op1=ALU.add,
+                )
+
         def interleave(s):
-            if s in S_INTER:
+            if s in S_INTER or s in G_INTER:
                 return
             src = wides[s] if GROUPS[s // NG][0] == "q" else raw[s]
             grps[s] = grp_pool.tile([P, GW, 4], BF16, name="grp", tag="grp", align_bytes=64)
@@ -258,6 +285,7 @@ def tile_gqa_flashattn_pa_kernel(
 
         accs = {}
         stats = {}
+        invs = {}
         work = {}
         sums = {}
 
@@ -280,7 +308,7 @@ def tile_gqa_flashattn_pa_kernel(
             accs[e] = acc
 
         def value_start_step(e):
-            users = [n for n in range(NNORM) if n % 4 == e % 4 and n not in V_ADD]
+            users = [n for n in range(NNORM) if n % 4 == e % 4 and n not in V_ADD + G_ADD]
             return max(users) + L_FIN + 1
 
         def value_passes(e, g_lo, g_hi):
@@ -301,12 +329,21 @@ def tile_gqa_flashattn_pa_kernel(
                     stop=(g == NG - 1),
                 )
 
+        def unit_stats(e):
+            st = stat_pool.tile([P, 2, 2, 3], F32, name="st", tag="st")
+            for j in range(2):
+                nc.vector.bn_stats(
+                    out=st[:, j, :, :].rearrange("p e c -> p (e c)"),
+                    in_=accs[e][:, 2 * j * HD : 2 * (j + 1) * HD].rearrange("p (e d) -> p d e", e=2),
+                )
+            stats[e] = st
+
         def head_sum(e, h):
             def run():
                 junk = junk_pool.tile([P, HD], BF16, name="junk", tag="junk")
                 nc.scalar.activation(
                     out=junk[:], in_=accs[e][:, h * HD : (h + 1) * HD], func=ACT.Identity, scale=-1.0 / HD,
-                    accum_out=stats[e][:, 4 + h : 5 + h],
+                    accum_out=stats[e][:, h // 2, h % 2, 1:2],
                 )
             return run
 
@@ -315,28 +352,35 @@ def tile_gqa_flashattn_pa_kernel(
                 junk = junk_pool.tile([P, HD], BF16, name="junk", tag="junk")
                 nc.scalar.activation(
                     out=junk[:], in_=accs[e][:, h * HD : (h + 1) * HD], func=ACT.Square,
-                    bias=stats[e][:, 4 + h : 5 + h], accum_out=stats[e][:, 8 + h : 9 + h],
+                    bias=stats[e][:, h // 2, h % 2, 1:2], accum_out=stats[e][:, h // 2, h % 2, 2:3],
                 )
             return run
 
-        def std_dev(e):
+        def scalar_stats(e):
+            stats[e] = stat_pool.tile([P, 2, 2, 3], F32, name="st", tag="st")
+            return [head_sum(e, h) for h in range(4)] + [head_sq(e, h) for h in range(4)]
+
+        def inv_std(e):
             def run():
+                inv = inv_pool.tile([P, 4], F32, name="inv", tag="inv")
                 nc.scalar.activation(
-                    out=stats[e][:, 12:16], in_=stats[e][:, 8:12], func=ACT.Abs_reciprocal_sqrt, scale=1.0 / HD, bias=EPS
+                    out=inv[:].rearrange("p (j e) -> p j e", j=2), in_=stats[e][:, :, :, 2], func=ACT.Abs_reciprocal_sqrt,
+                    scale=1.0 / HD, bias=EPS,
                 )
+                invs[e] = inv
             return run
 
         def epi_ab(e):
-            kind = GROUPS[e // NT][0]
+            kind = ("q", "k").index(GROUPS[e // NT][0])
             i = e % NT
             ab = ab_pool.tile([P, 4, 2, HD], F32, name="ab", tag="ab")
             for h in (3, 2, 1, 0):
                 nc.vector.scalar_tensor_tensor(
                     out=ab[:, h, :, :],
                     in0=accs[e][:, h * HD : (h + 1) * HD].unsqueeze(1).to_broadcast([P, 2, HD]),
-                    scalar=stats[e][:, 4 + h : 5 + h],
-                    in1=tabs[kind][0][:, i, :, :],
-                    op0=ALU.add,
+                    scalar=stats[e][:, h // 2, h % 2, 1:2],
+                    in1=ab_t[:, i, kind, :, :],
+                    op0=ALU.add if e in S_STAT else ALU.subtract,
                     op1=ALU.mult,
                 )
             work[e] = ab
@@ -362,6 +406,17 @@ def tile_gqa_flashattn_pa_kernel(
             )
             sums[e] = cc
 
+        def gpsimd_add(e):
+            ab = work[e]
+            cc = c_pool.tile([P, 4, HD], F32, name="cc", tag="cc")
+            nc.gpsimd.tensor_tensor(
+                out=cc[:].rearrange("p h (a d) -> p h a d", a=2),
+                in0=ab[:, :, 1, :].rearrange("p h (a d) -> p h a d", a=2),
+                in1=ab[:, :, 0, :].rearrange("p h (a d) -> p h a d", a=2)[:, :, ::-1, :],
+                op=ALU.add,
+            )
+            sums[e] = cc
+
         def out_view(e):
             kind, idx = GROUPS[e // NT]
             i = e % NT
@@ -369,12 +424,12 @@ def tile_gqa_flashattn_pa_kernel(
             return dram[0, 4 * idx : 4 * idx + 4, i * P : (i + 1) * P, :].rearrange("h p d -> p h d")
 
         def final(e):
-            kind = GROUPS[e // NT][0]
+            kind = ("q", "k").index(GROUPS[e // NT][0])
             i = e % NT
             o = o_pool.tile([P, 4, HD], F32, name="o", tag="o")
             for h in range(4):
                 nc.vector.scalar_tensor_tensor(
-                    out=o[:, h, :], in0=sums[e][:, h, :], scalar=stats[e][:, 12 + h : 13 + h], in1=tabs[kind][1][:, i, :],
+                    out=o[:, h, :], in0=sums[e][:, h, :], scalar=invs[e][:, h : h + 1], in1=c_t[:, i, kind, :],
                     op0=ALU.mult, op1=ALU.add,
                 )
             nc.sync.dma_start(out=out_view(e), in_=o[:])
@@ -387,13 +442,16 @@ def tile_gqa_flashattn_pa_kernel(
         def normed(e):
             return 0 <= e < NNORM
 
+        turn_cos_sin()
         done = {e: 0 for e in range(NNORM, NCHUNK)}
         full = []
         for s in range(-SA, NCHUNK + L_FIN + 2):
             if normed(s - L_MX):
                 unit_matmuls(s - L_MX)
-            if normed(s - L_ADD) and s - L_ADD not in V_ADD:
+            if normed(s - L_ADD) and s - L_ADD not in V_ADD + G_ADD:
                 tensor_add(s - L_ADD)
+            if s in TABLE_MM:
+                table_matmuls(TABLE_MM.index(s))
             for e in range(NNORM, NCHUNK):
                 ready = min(NG, s - (NNORM + 1))
                 if s >= value_start_step(e) and ready > done[e]:
@@ -401,42 +459,43 @@ def tile_gqa_flashattn_pa_kernel(
                     done[e] = ready
                     if ready == NG:
                         full.append(e)
-            if normed(s - L_ST):
-                stats[s - L_ST] = stat_pool.tile([P, 16], F32, name="st", tag="st")
-            fill = prep_scalar_ops(s + SA) if s + SA < NCHUNK else []
-            seq = list(fill[0:1])
-            if normed(s - L_ST - 1):
-                seq.append(std_dev(s - L_ST - 1))
+            fill = prep_scalar_ops(s + SA) if s + SA <= NCHUNK else []
+            seq = fill[0:1]
+            if normed(s - L_ADD):
+                seq.append(inv_std(s - L_ADD))
             seq.extend(fill[1:2])
-            if normed(s - L_ST):
-                seq.extend([head_sum(s - L_ST, h) for h in range(4)])
-                seq.extend(fill[2:4])
-                seq.extend([head_sq(s - L_ST, h) for h in range(4)])
-                seq.extend(fill[4:])
+            if normed(s - L_ST) and s - L_ST in S_STAT:
+                st_ops = scalar_stats(s - L_ST)
+                seq.extend(st_ops[0:4] + fill[2:4] + st_ops[4:8] + fill[4:])
             else:
                 seq.extend(fill[2:])
+            if s in TABLE_COPY:
+                seq.extend(table_copies(TABLE_COPY.index(s)))
             for op in seq:
                 op()
+            if normed(s - L_ADD) and s - L_ADD in G_ADD:
+                gpsimd_add(s - L_ADD)
+            if 0 <= s < NCHUNK:
+                gpsimd_interleave(s)
             for e in full:
                 copy_values(e)
             full.clear()
-            if s == Q_TABLES_AT:
-                build_tables("q")
-            if s == K_TABLES_AT:
-                build_tables("k")
+            if s == MIX_AT:
+                mix_matrices()
+                copy_cos_sin()
             if 0 <= s + VW < NCHUNK:
                 vector_widen(s + VW)
-            if normed(s - L_AB - 1) and s - L_AB - 1 in V_ADD:
-                vector_add(s - L_AB - 1)
+            if normed(s - L_ADD) and s - L_ADD in V_ADD:
+                vector_add(s - L_ADD)
             if 1 <= s <= NCHUNK:
                 interleave(s - 1)
             if 1 + X_LATE <= s <= NT + X_LATE:
                 x_quant(s - 1 - X_LATE)
+            if normed(s - L_FIN):
+                final(s - L_FIN)
             if normed(s - L_AB):
                 epi_ab(s - L_AB)
-            if normed(s - L_AB - 1) and s - L_AB - 1 in V_ADD:
-                final(s - L_AB - 1)
-            if normed(s - L_FIN) and s - L_FIN not in V_ADD:
-                final(s - L_FIN)
             if 1 <= s <= NCHUNK:
                 quantize(s - 1)
+            if normed(s - L_ST) and s - L_ST not in S_STAT:
+                unit_stats(s - L_ST)

@@ -229,8 +229,8 @@ def tile_gqa_flashattn_pa_kernel(
             def run():
                 src = wides[s] if GROUPS[s // NG][0] == "q" else raw[s]
                 nc.scalar.copy(
-                    out=grps[s][:].rearrange("p (c i) t -> p c t i", i=4),
-                    in_=src[:].rearrange("p t (c i) -> p c t i", i=4),
+                    out=grps[s][:].rearrange("p (c i) t -> p c t i", i=8),
+                    in_=src[:].rearrange("p t (c i) -> p c t i", i=8),
                 )
             return run
 
@@ -272,7 +272,7 @@ def tile_gqa_flashattn_pa_kernel(
             src = wides[s] if GROUPS[s // NG][0] == "q" else raw[s]
             grps[s] = grp_pool.tile([P, GW, 4], BF16, name="grp", tag="grp", align_bytes=64)
             nc.vector.tensor_copy(
-                out=grps[s][:].rearrange("p (c i) t -> p c t i", i=4), in_=src[:].rearrange("p t (c i) -> p c t i", i=4)
+                out=grps[s][:].rearrange("p (c i) t -> p c t i", i=8), in_=src[:].rearrange("p t (c i) -> p c t i", i=8)
             )
 
         def quantize(s):

@@ -25,30 +25,28 @@ GROUPS = (("q", 0), ("q", 1), ("q", 2), ("q", 3), ("k", 0), ("v", 0))
 NCHUNK = 24
 NNORM = 20
 SA = 2
-S_INTER = (12, 15, 17, 18, 20, 21, 23, )
-V_ADD = (13, 16, 17, 18, 19, )
-G_INTER = ()
-G_ADD = ()
-S_STAT = (1, 2, 3, 5, 6, 7, 9, 10, 11, 12, 13, 14, 15, 16, 17, 18, 19, )
-G_PIECES = 4
-HEAD_CHUNKS = 4
-V_EVERY = 0
+S_INTER = (9, 13, 16, 17, 18, 19, 20, 21, 22, 23)
+V_ADD = (10, 13, 16, 17, 18, 19)
+S_PAIR = ((0, 1), (1, 1), (2, 1), (3, 1), (4, 1), (5, 1), (6, 1), (7, 1), (8, 1), (9, 1), (10, 1), (11, 1), (12, 1), (13, 1), (14, 1), (15, 1), (16, 1), (17, 1), (18, 1), (19, 1))
+VP = (2, 2, 2, 2, 1, 1, 1, 1, 0, 0, 0, 0, 0, 0, 0, 0)
 VW = 1
-X_LATE = 1
-MIX_AT = 0
-TABLE_MM = (3, 4, 5, 6)
-TABLE_COPY = (3, 4, 5, 6)
+X_STEP = (0, 1, 2, 3)
+MIX_AT = 1
+TURN_AT = 1
+SWAP_AT = -1
+CST_AT = 3
+LOADS = ('w0', 'w1', 'g', 'x0', 'w2', 'x1', 'c', 'w3', 'x2', 'w4', 'x3')
+TABLE_MM = (4, 5, 6, 7)
 L_MX = 5
 L_ST = 5
 L_AB = 7
 L_ADD = 8
 L_FIN = 10
+L_FINV = 10
 
 
 def v_planes(s):
-    if s >= 16:
-        return ()
-    return (2, 3) if s < 4 else ((3,) if s < 8 else ())
+    return tuple(range(4 - VP[s], 4)) if s < 16 else ()
 
 
 def tile_gqa_flashattn_pa_kernel(
@@ -115,24 +113,29 @@ def tile_gqa_flashattn_pa_kernel(
             nc.sync.dma_start(out=t[:], in_=x[0, i * P : (i + 1) * P, :])
             xr[i] = t
 
-        load_chunk(0)
         gcol = const.tile([P, 4, 16], BF16, name="gcol", tag="gcol")
-        v = 0
-        with nc.allow_non_contiguous_dma(reason="four vectors of 128 values, one value to a partition"):
-            for vec in (q_gamma, k_gamma, q_beta, k_beta):
-                nc.sync.dma_start(out=gcol[:, v, 0:1], in_=vec.rearrange("(p o) -> p o", o=1))
-                v += 1
         cs = const.tile([P, 2, NT, HD], BF16, name="cs", tag="cs")
-        nc.sync.dma_start(out=cs[:, 0, :, :], in_=cos.rearrange("(i p) d -> p i d", p=P))
-        nc.sync.dma_start(out=cs[:, 1, :, :], in_=sin.rearrange("(i p) d -> p i d", p=P))
-        load_chunk(1)
-        load_x(0)
-        load_chunk(2)
-        load_x(1)
-        load_chunk(3)
-        load_x(2)
-        load_chunk(4)
-        load_x(3)
+
+        def load_vectors():
+            v = 0
+            with nc.allow_non_contiguous_dma(reason="four vectors of 128 values, one value to a partition"):
+                for vec in (q_gamma, k_gamma, q_beta, k_beta):
+                    nc.sync.dma_start(out=gcol[:, v, 0:1], in_=vec.rearrange("(p o) -> p o", o=1))
+                    v += 1
+
+        def load_cos_sin():
+            nc.sync.dma_start(out=cs[:, 0, :, :], in_=cos.rearrange("(i p) d -> p i d", p=P))
+            nc.sync.dma_start(out=cs[:, 1, :, :], in_=sin.rearrange("(i p) d -> p i d", p=P))
+
+        for what in LOADS:
+            if what == "g":
+                load_vectors()
+            elif what == "c":
+                load_cos_sin()
+            elif what[0] == "x":
+                load_x(int(what[1]))
+            else:
+                load_chunk(int(what[1]))
         for s in range(5, NCHUNK):
             load_chunk(s)
 
@@ -141,19 +144,22 @@ def tile_gqa_flashattn_pa_kernel(
         mix = const.tile([P, 4, 2, HD], BF16, name="mix", tag="mix")
         cst = const.tile([P, 2, NT, HD], BF16, name="cst", tag="cst")
         turned = []
+        swapped = []
 
         def turn_cos_sin():
+            ps = psum.tile([P, 2, NT, P], BF16, name="csp", tag="b6")
             for w in range(2):
-                ps = psum.tile([P, NT, P], BF16, name="csp", tag="b%d" % (6 + w))
                 for i in range(NT):
-                    nc.tensor.transpose(ps[:, i, :], cs[:, w, i, :], rmat[:, 0, :])
-                turned.append(ps)
-            swp = psum.tile([P, 4], F32, name="swp", tag="b5")
+                    nc.tensor.transpose(ps[:, w, i, :], cs[:, w, i, :], rmat[:, 0, :])
+            turned.append(ps)
+
+        def swap_vectors():
+            swp = psum.tile([P, 4], F32, name="swp", tag="b7")
             nc.tensor.matmul(out=swp[:], lhsT=rmat[:, 2, :], rhs=gcol[:, :, 0], start=True, stop=True)
-            turned.append(swp)
+            swapped.append(swp)
 
         def mix_matrices():
-            swp = turned[2]
+            swp = swapped[0]
             for k in range(2):
                 for j, block, col in (
                     (1, 0, gcol[:, k, 0:1]), (2, 0, gcol[:, 2 + k, 0:1]), (0, 1, swp[:, k : k + 1]), (3, 0, swp[:, 2 + k : 3 + k])
@@ -163,8 +169,7 @@ def tile_gqa_flashattn_pa_kernel(
                     )
 
         def copy_cos_sin():
-            for w in range(2):
-                nc.vector.tensor_copy(out=cst[:, w, :, :], in_=turned[w][:])
+            nc.vector.tensor_copy(out=cst[:].rearrange("p w i d -> p (w i d)"), in_=turned[0][:].rearrange("p w i d -> p (w i d)"))
 
         tab_ps = {}
 
@@ -229,8 +234,8 @@ def tile_gqa_flashattn_pa_kernel(
             def run():
                 src = wides[s] if GROUPS[s // NG][0] == "q" else raw[s]
                 nc.scalar.copy(
-                    out=grps[s][:].rearrange("p (c i) t -> p c t i", i=8),
-                    in_=src[:].rearrange("p t (c i) -> p c t i", i=8),
+                    out=grps[s][:].rearrange("p (c i) t -> p c t i", i=4),
+                    in_=src[:].rearrange("p t (c i) -> p c t i", i=4),
                 )
             return run
 
@@ -242,8 +247,9 @@ def tile_gqa_flashattn_pa_kernel(
             if s < NCHUNK and GROUPS[s // NG][0] == "q":
                 wides[s] = wide_pool.tile([P, 4, GW], BF16, name="wide", tag="wide")
                 ops.extend([widen_plane(s, t) for t in range(4) if t not in v_planes(s)])
-            if 1 + X_LATE <= s <= NT + X_LATE:
-                ops.extend([x_turn(s - 1 - X_LATE, half) for half in range(2)])
+            for i in range(NT):
+                if X_STEP[i] == s - SA:
+                    ops.extend([x_turn(i, half) for half in range(2)])
             return ops
 
         def vector_widen(s):
@@ -254,25 +260,13 @@ def tile_gqa_flashattn_pa_kernel(
                     scalar2=None, op0=ALU.mult,
                 )
 
-        def gpsimd_interleave(s):
-            if s not in G_INTER:
-                return
-            src = wides[s] if GROUPS[s // NG][0] == "q" else raw[s]
-            grps[s] = grp_pool.tile([P, GW, 4], BF16, name="grp", tag="grp", align_bytes=64)
-            w = GW // G_PIECES
-            for c in range(G_PIECES):
-                nc.gpsimd.tensor_scalar(
-                    out=grps[s][:, c * w : (c + 1) * w, :], in0=src[:, :, c * w : (c + 1) * w].rearrange("p t n -> p n t"),
-                    scalar1=1.0, scalar2=0.0, op0=ALU.mult, op1=ALU.add,
-                )
-
         def interleave(s):
-            if s in S_INTER or s in G_INTER:
+            if s in S_INTER:
                 return
             src = wides[s] if GROUPS[s // NG][0] == "q" else raw[s]
             grps[s] = grp_pool.tile([P, GW, 4], BF16, name="grp", tag="grp", align_bytes=64)
             nc.vector.tensor_copy(
-                out=grps[s][:].rearrange("p (c i) t -> p c t i", i=8), in_=src[:].rearrange("p t (c i) -> p c t i", i=8)
+                out=grps[s][:].rearrange("p (c i) t -> p c t i", i=4), in_=src[:].rearrange("p t (c i) -> p c t i", i=4)
             )
 
         def quantize(s):
@@ -308,7 +302,7 @@ def tile_gqa_flashattn_pa_kernel(
             accs[e] = acc
 
         def value_start_step(e):
-            users = [n for n in range(NNORM) if n % 4 == e % 4 and n not in V_ADD + G_ADD]
+            users = [n for n in range(NNORM) if n % 4 == e % 4 and n not in V_ADD]
             return max(users) + L_FIN + 1
 
         def value_passes(e, g_lo, g_hi):
@@ -329,21 +323,20 @@ def tile_gqa_flashattn_pa_kernel(
                     stop=(g == NG - 1),
                 )
 
-        def unit_stats(e):
-            st = stat_pool.tile([P, 2, 2, 3], F32, name="st", tag="st")
-            for j in range(2):
-                nc.vector.bn_stats(
-                    out=st[:, j, :, :].rearrange("p e c -> p (e c)"),
-                    in_=accs[e][:, 2 * j * HD : 2 * (j + 1) * HD].rearrange("p (e d) -> p d e", e=2),
-                )
-            stats[e] = st
+        def vector_stats(e, j):
+            st = stat_pool.tile([P, 2, 3], F32, name="st", tag="st%d" % j)
+            nc.vector.bn_stats(
+                out=st[:].rearrange("p e c -> p (e c)"),
+                in_=accs[e][:, 2 * j * HD : 2 * (j + 1) * HD].rearrange("p (e d) -> p d e", e=2),
+            )
+            stats[(e, j)] = st
 
         def head_sum(e, h):
             def run():
                 junk = junk_pool.tile([P, HD], BF16, name="junk", tag="junk")
                 nc.scalar.activation(
                     out=junk[:], in_=accs[e][:, h * HD : (h + 1) * HD], func=ACT.Identity, scale=-1.0 / HD,
-                    accum_out=stats[e][:, h // 2, h % 2, 1:2],
+                    accum_out=stats[(e, h // 2)][:, h % 2, 1:2],
                 )
             return run
 
@@ -352,21 +345,25 @@ def tile_gqa_flashattn_pa_kernel(
                 junk = junk_pool.tile([P, HD], BF16, name="junk", tag="junk")
                 nc.scalar.activation(
                     out=junk[:], in_=accs[e][:, h * HD : (h + 1) * HD], func=ACT.Square,
-                    bias=stats[e][:, h // 2, h % 2, 1:2], accum_out=stats[e][:, h // 2, h % 2, 2:3],
+                    bias=stats[(e, h // 2)][:, h % 2, 1:2], accum_out=stats[(e, h // 2)][:, h % 2, 2:3],
                 )
             return run
 
         def scalar_stats(e):
-            stats[e] = stat_pool.tile([P, 2, 2, 3], F32, name="st", tag="st")
-            return [head_sum(e, h) for h in range(4)] + [head_sq(e, h) for h in range(4)]
+            heads = [h for h in range(4) if (e, h // 2) in S_PAIR]
+            for j in range(2):
+                if (e, j) in S_PAIR:
+                    stats[(e, j)] = stat_pool.tile([P, 2, 3], F32, name="st", tag="st%d" % j)
+            return [head_sum(e, h) for h in heads], [head_sq(e, h) for h in heads]
 
         def inv_std(e):
             def run():
                 inv = inv_pool.tile([P, 4], F32, name="inv", tag="inv")
-                nc.scalar.activation(
-                    out=inv[:].rearrange("p (j e) -> p j e", j=2), in_=stats[e][:, :, :, 2], func=ACT.Abs_reciprocal_sqrt,
-                    scale=1.0 / HD, bias=EPS,
-                )
+                for j in range(2):
+                    nc.scalar.activation(
+                        out=inv[:, 2 * j : 2 * j + 2], in_=stats[(e, j)][:, :, 2], func=ACT.Abs_reciprocal_sqrt,
+                        scale=1.0 / HD, bias=EPS,
+                    )
                 invs[e] = inv
             return run
 
@@ -378,9 +375,9 @@ def tile_gqa_flashattn_pa_kernel(
                 nc.vector.scalar_tensor_tensor(
                     out=ab[:, h, :, :],
                     in0=accs[e][:, h * HD : (h + 1) * HD].unsqueeze(1).to_broadcast([P, 2, HD]),
-                    scalar=stats[e][:, h // 2, h % 2, 1:2],
+                    scalar=stats[(e, h // 2)][:, h % 2, 1:2],
                     in1=ab_t[:, i, kind, :, :],
-                    op0=ALU.add if e in S_STAT else ALU.subtract,
+                    op0=ALU.add if (e, h // 2) in S_PAIR else ALU.subtract,
                     op1=ALU.mult,
                 )
             work[e] = ab
@@ -399,17 +396,6 @@ def tile_gqa_flashattn_pa_kernel(
             ab = work[e]
             cc = c_pool.tile([P, 4, HD], F32, name="cc", tag="cc")
             nc.vector.tensor_tensor(
-                out=cc[:].rearrange("p h (a d) -> p h a d", a=2),
-                in0=ab[:, :, 1, :].rearrange("p h (a d) -> p h a d", a=2),
-                in1=ab[:, :, 0, :].rearrange("p h (a d) -> p h a d", a=2)[:, :, ::-1, :],
-                op=ALU.add,
-            )
-            sums[e] = cc
-
-        def gpsimd_add(e):
-            ab = work[e]
-            cc = c_pool.tile([P, 4, HD], F32, name="cc", tag="cc")
-            nc.gpsimd.tensor_tensor(
                 out=cc[:].rearrange("p h (a d) -> p h a d", a=2),
                 in0=ab[:, :, 1, :].rearrange("p h (a d) -> p h a d", a=2),
                 in1=ab[:, :, 0, :].rearrange("p h (a d) -> p h a d", a=2)[:, :, ::-1, :],
@@ -442,13 +428,12 @@ def tile_gqa_flashattn_pa_kernel(
         def normed(e):
             return 0 <= e < NNORM
 
-        turn_cos_sin()
         done = {e: 0 for e in range(NNORM, NCHUNK)}
         full = []
         for s in range(-SA, NCHUNK + L_FIN + 2):
             if normed(s - L_MX):
                 unit_matmuls(s - L_MX)
-            if normed(s - L_ADD) and s - L_ADD not in V_ADD + G_ADD:
+            if normed(s - L_ADD) and s - L_ADD not in V_ADD:
                 tensor_add(s - L_ADD)
             if s in TABLE_MM:
                 table_matmuls(TABLE_MM.index(s))
@@ -464,24 +449,22 @@ def tile_gqa_flashattn_pa_kernel(
             if normed(s - L_ADD):
                 seq.append(inv_std(s - L_ADD))
             seq.extend(fill[1:2])
-            if normed(s - L_ST) and s - L_ST in S_STAT:
-                st_ops = scalar_stats(s - L_ST)
-                seq.extend(st_ops[0:4] + fill[2:4] + st_ops[4:8] + fill[4:])
-            else:
-                seq.extend(fill[2:])
-            if s in TABLE_COPY:
-                seq.extend(table_copies(TABLE_COPY.index(s)))
+            sums_ops, sq_ops = scalar_stats(s - L_ST) if normed(s - L_ST) else ([], [])
+            seq.extend(sums_ops + fill[2:4] + sq_ops + fill[4:])
+            if s in TABLE_MM:
+                seq.extend(table_copies(TABLE_MM.index(s)))
+            if s == SWAP_AT:
+                swap_vectors()
             for op in seq:
                 op()
-            if normed(s - L_ADD) and s - L_ADD in G_ADD:
-                gpsimd_add(s - L_ADD)
-            if 0 <= s < NCHUNK:
-                gpsimd_interleave(s)
+            if s == TURN_AT:
+                turn_cos_sin()
             for e in full:
                 copy_values(e)
             full.clear()
             if s == MIX_AT:
                 mix_matrices()
+            if s == CST_AT:
                 copy_cos_sin()
             if 0 <= s + VW < NCHUNK:
                 vector_widen(s + VW)
@@ -489,13 +472,18 @@ def tile_gqa_flashattn_pa_kernel(
                 vector_add(s - L_ADD)
             if 1 <= s <= NCHUNK:
                 interleave(s - 1)
-            if 1 + X_LATE <= s <= NT + X_LATE:
-                x_quant(s - 1 - X_LATE)
-            if normed(s - L_FIN):
+            for i in range(NT):
+                if X_STEP[i] + 2 == s:
+                    x_quant(i)
+            if normed(s - L_FINV) and s - L_FINV in V_ADD:
+                final(s - L_FINV)
+            if normed(s - L_FIN) and s - L_FIN not in V_ADD:
                 final(s - L_FIN)
             if normed(s - L_AB):
                 epi_ab(s - L_AB)
             if 1 <= s <= NCHUNK:
                 quantize(s - 1)
-            if normed(s - L_ST) and s - L_ST not in S_STAT:
-                unit_stats(s - L_ST)
+            if normed(s - L_ST):
+                for j in range(2):
+                    if (s - L_ST, j) not in S_PAIR:
+                        vector_stats(s - L_ST, j)

@@ -27,7 +27,7 @@ NNORM = 20
 SA = 2
 S_INTER = (9, 13, 16, 17, 18, 19, 20, 21, 22, 23)
 V_ADD = (10, 13, 16, 17, 18, 19)
-S_PAIR = ((0, 1), (1, 1), (2, 1), (3, 1), (4, 1), (5, 1), (6, 1), (7, 1), (8, 1), (9, 1), (10, 1), (11, 1), (12, 1), (13, 1), (14, 1), (15, 1), (16, 1), (17, 1), (18, 1), (19, 1))
+S_PAIR = ((1, 0), (1, 1), (3, 0), (3, 1), (5, 0), (5, 1), (7, 0), (7, 1), (9, 0), (9, 1), (11, 0), (11, 1), (13, 0), (13, 1), (15, 0), (15, 1), (16, 0), (16, 1), (17, 0), (17, 1), (18, 0), (18, 1), (19, 0), (19, 1))
 VP = (2, 2, 2, 2, 1, 1, 1, 1, 0, 0, 0, 0, 0, 0, 0, 0)
 VW = 1
 X_STEP = (0, 1, 2, 3)
@@ -43,6 +43,8 @@ L_AB = 7
 L_ADD = 8
 L_FIN = 10
 L_FINV = 10
+EARLY = ()
+FIN_EARLY = ()
 
 
 def v_planes(s):
@@ -58,7 +60,7 @@ def tile_gqa_flashattn_pa_kernel(
         bytes_pool = ctx.enter_context(tc.tile_pool(name="bytes", bufs=16))
         raw_pool = ctx.enter_context(tc.tile_pool(name="raw", bufs=8))
         x_pool = ctx.enter_context(tc.tile_pool(name="xraw", bufs=4))
-        gx_pool = ctx.enter_context(tc.tile_pool(name="gx", bufs=8))
+        gx_pool = ctx.enter_context(tc.tile_pool(name="gx", bufs=4))
         wide_pool = ctx.enter_context(tc.tile_pool(name="wide", bufs=6))
         grp_pool = ctx.enter_context(tc.tile_pool(name="grp", bufs=5))
         code_pool = ctx.enter_context(tc.tile_pool(name="codes", bufs=10))
@@ -202,20 +204,21 @@ def tile_gqa_flashattn_pa_kernel(
                     g = 2 * half + gl
                     for u in range(2):
                         nc.tensor.transpose(xt[:, gl, u, :], words[:, 256 * g + u : 256 * (g + 1) : 2], ident[:])
-                gx = gx_pool.tile([P, 2, P, 4], BF16, name="gx", tag="gx", align_bytes=64)
-                dst = gx[:].rearrange("p g r j -> p (g r j)").bitcast(F32).rearrange("p (g r u) -> p g r u", g=2, u=2)
-                nc.scalar.copy(out=dst, in_=xt[:].rearrange("p g u r -> p g r u"))
-                gxs[(i, half)] = gx
+                if half == 0:
+                    gxs[i] = gx_pool.tile([P, NG, P, 4], BF16, name="gx", tag="gx", align_bytes=64)
+                dst = gxs[i][:, 2 * half : 2 * half + 2, :, :].rearrange("p g r j -> p (g r j)").bitcast(F32)
+                nc.scalar.copy(
+                    out=dst.rearrange("p (g r u) -> p g r u", g=2, u=2), in_=xt[:].rearrange("p g u r -> p g r u")
+                )
             return run
 
         def x_quant(i):
-            for half in range(2):
-                lo = (NG * i + 2 * half) * P
-                nc.vector.quantize_mx(
-                    out=xc[:, lo : lo + 2 * P].bitcast(FP8X4),
-                    scales=xs[:, lo : lo + 2 * P],
-                    in_=gxs[(i, half)][:].rearrange("p g r j -> p (g r j)"),
-                )
+            lo = NG * i * P
+            nc.vector.quantize_mx(
+                out=xc[:, lo : lo + NG * P].bitcast(FP8X4),
+                scales=xs[:, lo : lo + NG * P],
+                in_=gxs[i][:].rearrange("p g r j -> p (g r j)"),
+            )
 
         wides = {}
         grps = {}
@@ -303,7 +306,7 @@ def tile_gqa_flashattn_pa_kernel(
 
         def value_start_step(e):
             users = [n for n in range(NNORM) if n % 4 == e % 4 and n not in V_ADD]
-            return max(users) + L_FIN + 1
+            return max(users + [0]) + L_FIN + 1
 
         def value_passes(e, g_lo, g_hi):
             c = e // NT
@@ -324,19 +327,17 @@ def tile_gqa_flashattn_pa_kernel(
                 )
 
         def vector_stats(e, j):
-            st = stat_pool.tile([P, 2, 3], F32, name="st", tag="st%d" % j)
             nc.vector.bn_stats(
-                out=st[:].rearrange("p e c -> p (e c)"),
+                out=stats[e][:, j, :, :].rearrange("p e c -> p (e c)"),
                 in_=accs[e][:, 2 * j * HD : 2 * (j + 1) * HD].rearrange("p (e d) -> p d e", e=2),
             )
-            stats[(e, j)] = st
 
         def head_sum(e, h):
             def run():
                 junk = junk_pool.tile([P, HD], BF16, name="junk", tag="junk")
                 nc.scalar.activation(
                     out=junk[:], in_=accs[e][:, h * HD : (h + 1) * HD], func=ACT.Identity, scale=-1.0 / HD,
-                    accum_out=stats[(e, h // 2)][:, h % 2, 1:2],
+                    accum_out=stats[e][:, h // 2, h % 2, 1:2],
                 )
             return run
 
@@ -345,25 +346,21 @@ def tile_gqa_flashattn_pa_kernel(
                 junk = junk_pool.tile([P, HD], BF16, name="junk", tag="junk")
                 nc.scalar.activation(
                     out=junk[:], in_=accs[e][:, h * HD : (h + 1) * HD], func=ACT.Square,
-                    bias=stats[(e, h // 2)][:, h % 2, 1:2], accum_out=stats[(e, h // 2)][:, h % 2, 2:3],
+                    bias=stats[e][:, h // 2, h % 2, 1:2], accum_out=stats[e][:, h // 2, h % 2, 2:3],
                 )
             return run
 
         def scalar_stats(e):
             heads = [h for h in range(4) if (e, h // 2) in S_PAIR]
-            for j in range(2):
-                if (e, j) in S_PAIR:
-                    stats[(e, j)] = stat_pool.tile([P, 2, 3], F32, name="st", tag="st%d" % j)
             return [head_sum(e, h) for h in heads], [head_sq(e, h) for h in heads]
 
         def inv_std(e):
             def run():
                 inv = inv_pool.tile([P, 4], F32, name="inv", tag="inv")
-                for j in range(2):
-                    nc.scalar.activation(
-                        out=inv[:, 2 * j : 2 * j + 2], in_=stats[(e, j)][:, :, 2], func=ACT.Abs_reciprocal_sqrt,
-                        scale=1.0 / HD, bias=EPS,
-                    )
+                nc.scalar.activation(
+                    out=inv[:].rearrange("p (j e) -> p j e", j=2), in_=stats[e][:, :, :, 2], func=ACT.Abs_reciprocal_sqrt,
+                    scale=1.0 / HD, bias=EPS,
+                )
                 invs[e] = inv
             return run
 
@@ -375,7 +372,7 @@ def tile_gqa_flashattn_pa_kernel(
                 nc.vector.scalar_tensor_tensor(
                     out=ab[:, h, :, :],
                     in0=accs[e][:, h * HD : (h + 1) * HD].unsqueeze(1).to_broadcast([P, 2, HD]),
-                    scalar=stats[(e, h // 2)][:, h % 2, 1:2],
+                    scalar=stats[e][:, h // 2, h % 2, 1:2],
                     in1=ab_t[:, i, kind, :, :],
                     op0=ALU.add if (e, h // 2) in S_PAIR else ALU.subtract,
                     op1=ALU.mult,
@@ -428,13 +425,17 @@ def tile_gqa_flashattn_pa_kernel(
         def normed(e):
             return 0 <= e < NNORM
 
+        def units(s, lag):
+            return [e for e in range(NNORM) if e - (1 if e in EARLY else 0) + lag == s]
+
         done = {e: 0 for e in range(NNORM, NCHUNK)}
         full = []
         for s in range(-SA, NCHUNK + L_FIN + 2):
-            if normed(s - L_MX):
-                unit_matmuls(s - L_MX)
-            if normed(s - L_ADD) and s - L_ADD not in V_ADD:
-                tensor_add(s - L_ADD)
+            for e in units(s, L_MX):
+                unit_matmuls(e)
+            for e in units(s, L_ADD):
+                if e not in V_ADD:
+                    tensor_add(e)
             if s in TABLE_MM:
                 table_matmuls(TABLE_MM.index(s))
             for e in range(NNORM, NCHUNK):
@@ -446,10 +447,15 @@ def tile_gqa_flashattn_pa_kernel(
                         full.append(e)
             fill = prep_scalar_ops(s + SA) if s + SA <= NCHUNK else []
             seq = fill[0:1]
-            if normed(s - L_ADD):
-                seq.append(inv_std(s - L_ADD))
+            for e in units(s, L_ADD):
+                seq.append(inv_std(e))
             seq.extend(fill[1:2])
-            sums_ops, sq_ops = scalar_stats(s - L_ST) if normed(s - L_ST) else ([], [])
+            sums_ops, sq_ops = [], []
+            for e in units(s, L_ST):
+                stats[e] = stat_pool.tile([P, 2, 2, 3], F32, name="st", tag="st")
+                a_ops, b_ops = scalar_stats(e)
+                sums_ops.extend(a_ops)
+                sq_ops.extend(b_ops)
             seq.extend(sums_ops + fill[2:4] + sq_ops + fill[4:])
             if s in TABLE_MM:
                 seq.extend(table_copies(TABLE_MM.index(s)))
@@ -468,22 +474,22 @@ def tile_gqa_flashattn_pa_kernel(
                 copy_cos_sin()
             if 0 <= s + VW < NCHUNK:
                 vector_widen(s + VW)
-            if normed(s - L_ADD) and s - L_ADD in V_ADD:
-                vector_add(s - L_ADD)
+            for e in units(s, L_ADD):
+                if e in V_ADD:
+                    vector_add(e)
             if 1 <= s <= NCHUNK:
                 interleave(s - 1)
             for i in range(NT):
                 if X_STEP[i] + 2 == s:
                     x_quant(i)
-            if normed(s - L_FINV) and s - L_FINV in V_ADD:
-                final(s - L_FINV)
-            if normed(s - L_FIN) and s - L_FIN not in V_ADD:
-                final(s - L_FIN)
-            if normed(s - L_AB):
-                epi_ab(s - L_AB)
+            for e in range(NNORM):
+                if e + (L_FINV if e in V_ADD else L_FIN) - (1 if e in FIN_EARLY else 0) == s:
+                    final(e)
+            for e in units(s, L_AB):
+                epi_ab(e)
             if 1 <= s <= NCHUNK:
                 quantize(s - 1)
-            if normed(s - L_ST):
+            for e in units(s, L_ST):
                 for j in range(2):
-                    if (s - L_ST, j) not in S_PAIR:
-                        vector_stats(s - L_ST, j)
+                    if (e, j) not in S_PAIR:
+                        vector_stats(e, j)

@@ -25,17 +25,22 @@ GROUPS = (("q", 0), ("q", 1), ("q", 2), ("q", 3), ("k", 0), ("v", 0))
 NCHUNK = 24
 NNORM = 20
 SA = 2
-S_INTER = (9, 13, 16, 17, 18, 19, 20, 21, 22, 23)
+S_INTER = (10, 14, 16, 17, 18, 19, 20, 21, 22, 23)
 V_ADD = (10, 13, 16, 17, 18, 19)
 S_PAIR = ((1, 0), (1, 1), (3, 0), (3, 1), (5, 0), (5, 1), (7, 0), (7, 1), (9, 0), (9, 1), (11, 0), (11, 1), (13, 0), (13, 1), (15, 0), (15, 1), (16, 0), (16, 1), (17, 0), (17, 1), (18, 0), (18, 1), (19, 0), (19, 1))
 VP = (2, 2, 2, 2, 1, 1, 1, 1, 0, 0, 0, 0, 0, 0, 0, 0)
 VW = 1
-X_STEP = (0, 1, 2, 3)
-MIX_AT = 1
+W_POS = 1
+SPLIT_FROM = 19
+G_INTER = ()
+G_PIECES = 4
+G_AHEAD = 0
+X_STEP = (0, 1, 2, 4)
+MIX_AT = 3
 TURN_AT = 1
-SWAP_AT = -1
+SWAP_AT = 0
 CST_AT = 3
-LOADS = ('w0', 'w1', 'g', 'x0', 'w2', 'x1', 'c', 'w3', 'x2', 'w4', 'x3')
+LOADS = ('s0', 'w0', 's1', 'w1', 's2', 'w2', 'x0', 'g', 's3', 'x1', 'w3', 'w4', 'c', 'x2', 'x3')
 TABLE_MM = (4, 5, 6, 7)
 L_MX = 5
 L_ST = 5
@@ -88,11 +93,12 @@ def tile_gqa_flashattn_pa_kernel(
         ident = const.tile([P, P], F32, name="ident", tag="ident")
         make_identity(nc, ident[:])
 
-        wsc = const.tile([P, NG * 4], F32, name="wsc", tag="wsc")
-        nc.sync.dma_start(
-            out=wsc[:].rearrange("p (g t) -> p g t", g=NG),
-            in_=wq_scale.rearrange("(g p t) o -> p g (t o)", p=P, t=4),
-        )
+        wsc = const.tile([P, NG, 8], F32, name="wsc", tag="wsc")
+        wsc_v = wq_scale.rearrange("(g p t) o -> g p (t o)", p=P, t=4)
+
+        def load_scales(g):
+            nc.sync.dma_start(out=wsc[:, g, 0:4], in_=wsc_v[g])
+
         wq_v = wq_bytes.rearrange("(g p t) n -> g p t n", p=P, t=4)
         wk_v = wk.rearrange("(g p t) n -> g p t n", p=P, t=4)
         wv_v = wv.rearrange("(g p t) n -> g p t n", p=P, t=4)
@@ -134,6 +140,8 @@ def tile_gqa_flashattn_pa_kernel(
                 load_vectors()
             elif what == "c":
                 load_cos_sin()
+            elif what[0] == "s":
+                load_scales(int(what[1]))
             elif what[0] == "x":
                 load_x(int(what[1]))
             else:
@@ -229,7 +237,7 @@ def tile_gqa_flashattn_pa_kernel(
                 g = s % NG
                 nc.scalar.activation(
                     out=wides[s][:, t, :], in_=raw[s][:, t, :].bitcast(FP8), func=ACT.Copy,
-                    scale=wsc[:, 4 * g + t : 4 * g + t + 1],
+                    scale=wsc[:, g, t : t + 1],
                 )
             return run
 
@@ -259,12 +267,22 @@ def tile_gqa_flashattn_pa_kernel(
             g = s % NG
             for t in v_planes(s):
                 nc.vector.tensor_scalar(
-                    out=wides[s][:, t, :], in0=raw[s][:, t, :].bitcast(FP8), scalar1=wsc[:, 4 * g + t : 4 * g + t + 1],
+                    out=wides[s][:, t, :], in0=raw[s][:, t, :].bitcast(FP8), scalar1=wsc[:, g, t : t + 1],
                     scalar2=None, op0=ALU.mult,
                 )
 
+        def gpsimd_interleave(s):
+            src = wides[s] if GROUPS[s // NG][0] == "q" else raw[s]
+            grps[s] = grp_pool.tile([P, GW, 4], BF16, name="grp", tag="grp", align_bytes=64)
+            w = GW // G_PIECES
+            for c in range(G_PIECES):
+                nc.gpsimd.tensor_scalar(
+                    out=grps[s][:, c * w : (c + 1) * w, :], in0=src[:, :, c * w : (c + 1) * w].rearrange("p t n -> p n t"),
+                    scalar1=1.0, scalar2=0.0, op0=ALU.mult, op1=ALU.add,
+                )
+
         def interleave(s):
-            if s in S_INTER:
+            if s in S_INTER or s in G_INTER:
                 return
             src = wides[s] if GROUPS[s // NG][0] == "q" else raw[s]
             grps[s] = grp_pool.tile([P, GW, 4], BF16, name="grp", tag="grp", align_bytes=64)
@@ -415,7 +433,10 @@ def tile_gqa_flashattn_pa_kernel(
                     out=o[:, h, :], in0=sums[e][:, h, :], scalar=invs[e][:, h : h + 1], in1=c_t[:, i, kind, :],
                     op0=ALU.mult, op1=ALU.add,
                 )
-            nc.sync.dma_start(out=out_view(e), in_=o[:])
+                if e >= SPLIT_FROM and h % 2 == 1:
+                    nc.sync.dma_start(out=out_view(e)[:, h - 1 : h + 1, :], in_=o[:, h - 1 : h + 1, :])
+            if e < SPLIT_FROM:
+                nc.sync.dma_start(out=out_view(e), in_=o[:])
 
         def copy_values(e):
             o = o_pool.tile([P, 4, HD], F32, name="o", tag="o")
@@ -463,6 +484,8 @@ def tile_gqa_flashattn_pa_kernel(
                 swap_vectors()
             for op in seq:
                 op()
+            if s + G_AHEAD in G_INTER:
+                gpsimd_interleave(s + G_AHEAD)
             if s == TURN_AT:
                 turn_cos_sin()
             for e in full:
@@ -472,13 +495,15 @@ def tile_gqa_flashattn_pa_kernel(
                 mix_matrices()
             if s == CST_AT:
                 copy_cos_sin()
-            if 0 <= s + VW < NCHUNK:
+            if W_POS == 0 and 0 <= s + VW < NCHUNK:
                 vector_widen(s + VW)
             for e in units(s, L_ADD):
                 if e in V_ADD:
                     vector_add(e)
             if 1 <= s <= NCHUNK:
                 interleave(s - 1)
+            if W_POS == 1 and 0 <= s + VW < NCHUNK:
+                vector_widen(s + VW)
             for i in range(NT):
                 if X_STEP[i] + 2 == s:
                     x_quant(i)
@@ -487,8 +512,12 @@ def tile_gqa_flashattn_pa_kernel(
                     final(e)
             for e in units(s, L_AB):
                 epi_ab(e)
+            if W_POS == 2 and 0 <= s + VW < NCHUNK:
+                vector_widen(s + VW)
             if 1 <= s <= NCHUNK:
                 quantize(s - 1)
+            if W_POS == 3 and 0 <= s + VW < NCHUNK:
+                vector_widen(s + VW)
             for e in units(s, L_ST):
                 for j in range(2):
                     if (e, j) not in S_PAIR:

@@ -27,21 +27,25 @@ NNORM = 20
 SA = 2
 S_INTER = (10, 14, 16, 17, 18, 19, 20, 21, 22, 23)
 V_ADD = (10, 13, 16, 17, 18, 19)
-S_PAIR = ((1, 0), (1, 1), (3, 0), (3, 1), (5, 0), (5, 1), (7, 0), (7, 1), (9, 0), (9, 1), (11, 0), (11, 1), (13, 0), (13, 1), (15, 0), (15, 1), (16, 0), (16, 1), (17, 0), (17, 1), (18, 0), (18, 1), (19, 0), (19, 1))
+S_PAIR = ((1, 0), (1, 1), (3, 0), (3, 1), (5, 0), (5, 1), (7, 0), (7, 1), (9, 0), (9, 1), (11, 0), (11, 1), (13, 0), (13, 1), (15, 0), (15, 1), (17, 0), (17, 1), (18, 0), (18, 1), (19, 0), (19, 1))
 VP = (2, 2, 2, 2, 1, 1, 1, 1, 0, 0, 0, 0, 0, 0, 0, 0)
 VW = 1
 W_POS = 1
+ADD_LAST = 99
+CST_S = 0
+XB = 2
+XN = 4
 SPLIT_FROM = 19
 G_INTER = ()
 G_PIECES = 4
 G_AHEAD = 0
 X_STEP = (0, 1, 2, 4)
-MIX_AT = 3
-TURN_AT = 1
-SWAP_AT = 0
-CST_AT = 3
-LOADS = ('s0', 'w0', 's1', 'w1', 's2', 'w2', 'x0', 'g', 's3', 'x1', 'w3', 'w4', 'c', 'x2', 'x3')
-TABLE_MM = (4, 5, 6, 7)
+MIX_AT = 4
+TURN_AT = 3
+SWAP_AT = 3
+CST_AT = 4
+LOADS = ('s0', 'a0', 'b0', 's1', 'w1', 's2', 'w2', 'x0', 's3', 'w3', 'x1', 'w4', 'x2', 'c', 'w5', 'g', 'x3')
+TABLE_MM = (5, 6, 7, 8)
 L_MX = 5
 L_ST = 5
 L_AB = 7
@@ -49,11 +53,11 @@ L_ADD = 8
 L_FIN = 10
 L_FINV = 10
 EARLY = ()
-FIN_EARLY = ()
+FIN_EARLY = (16, 17, 18, 19)
 
 
 def v_planes(s):
-    return tuple(range(4 - VP[s], 4)) if s < 16 else ()
+    return tuple(range(4 - VP[s], 4)) if s < len(VP) and GROUPS[s // NG][0] == "q" else ()
 
 
 def tile_gqa_flashattn_pa_kernel(
@@ -116,6 +120,13 @@ def tile_gqa_flashattn_pa_kernel(
                 nc.sync.dma_start(out=t[:], in_=(wk_v if kind == "k" else wv_v)[g])
             raw[s] = t
 
+        def load_half_chunk(s, half):
+            if half == 0:
+                raw[s] = bytes_pool.tile([P, 4, GW], U8, name="wq_bytes", tag="wq_bytes")
+            nc.sync.dma_start(
+                out=raw[s][:, 2 * half : 2 * half + 2, :], in_=wq_v[s % NG][:, 2 * half : 2 * half + 2, 0:GW]
+            )
+
         def load_x(i):
             t = x_pool.tile([P, 2048], BF16, name="xraw", tag="xraw")
             nc.sync.dma_start(out=t[:], in_=x[0, i * P : (i + 1) * P, :])
@@ -140,14 +151,17 @@ def tile_gqa_flashattn_pa_kernel(
                 load_vectors()
             elif what == "c":
                 load_cos_sin()
+            elif what[0] in "ab":
+                load_half_chunk(int(what[1]), "ab".index(what[0]))
             elif what[0] == "s":
                 load_scales(int(what[1]))
             elif what[0] == "x":
                 load_x(int(what[1]))
             else:
                 load_chunk(int(what[1]))
-        for s in range(5, NCHUNK):
-            load_chunk(s)
+        for s in range(NCHUNK):
+            if s not in raw:
+                load_chunk(s)
 
         ab_t = const.tile([P, NT, 2, 2, HD], F32, name="ab_t", tag="ab_t")
         c_t = const.tile([P, NT, 2, HD], F32, name="c_t", tag="c_t")
@@ -179,7 +193,7 @@ def tile_gqa_flashattn_pa_kernel(
                     )
 
         def copy_cos_sin():
-            nc.vector.tensor_copy(out=cst[:].rearrange("p w i d -> p (w i d)"), in_=turned[0][:].rearrange("p w i d -> p (w i d)"))
+            (nc.scalar.copy if CST_S else nc.vector.tensor_copy)(out=cst[:].rearrange("p w i d -> p (w i d)"), in_=turned[0][:].rearrange("p w i d -> p (w i d)"))
 
         tab_ps = {}
 
@@ -207,7 +221,7 @@ def tile_gqa_flashattn_pa_kernel(
         def x_turn(i, half):
             def run():
                 words = xr[i][:].bitcast(F32)
-                xt = psum.tile([P, 2, 2, P], F32, name="xt", tag="b%d" % ((2 * i + half) % 6))
+                xt = psum.tile([P, 2, 2, P], F32, name="xt", tag="b%d" % (XB + (2 * i + half) % XN))
                 for gl in range(2):
                     g = 2 * half + gl
                     for u in range(2):
@@ -455,7 +469,7 @@ def tile_gqa_flashattn_pa_kernel(
             for e in units(s, L_MX):
                 unit_matmuls(e)
             for e in units(s, L_ADD):
-                if e not in V_ADD:
+                if e not in V_ADD and s < ADD_LAST:
                     tensor_add(e)
             if s in TABLE_MM:
                 table_matmuls(TABLE_MM.index(s))
@@ -466,6 +480,9 @@ def tile_gqa_flashattn_pa_kernel(
                     done[e] = ready
                     if ready == NG:
                         full.append(e)
+            for e in units(s, L_ADD):
+                if e not in V_ADD and s >= ADD_LAST:
+                    tensor_add(e)
             fill = prep_scalar_ops(s + SA) if s + SA <= NCHUNK else []
             seq = fill[0:1]
             for e in units(s, L_ADD):
@@ -484,6 +501,8 @@ def tile_gqa_flashattn_pa_kernel(
                 swap_vectors()
             for op in seq:
                 op()
+            if s == CST_AT and CST_S:
+                copy_cos_sin()
             if s + G_AHEAD in G_INTER:
                 gpsimd_interleave(s + G_AHEAD)
             if s == TURN_AT:
@@ -493,7 +512,7 @@ def tile_gqa_flashattn_pa_kernel(
             full.clear()
             if s == MIX_AT:
                 mix_matrices()
-            if s == CST_AT:
+            if s == CST_AT and not CST_S:
                 copy_cos_sin()
             if W_POS == 0 and 0 <= s + VW < NCHUNK:
                 vector_widen(s + VW)

@@ -27,10 +27,11 @@ NNORM = 20
 SA = 2
 S_INTER = (10, 14, 16, 17, 18, 19, 20, 21, 22, 23)
 V_ADD = (10, 13, 16, 17, 18, 19)
-S_PAIR = ((1, 0), (1, 1), (3, 0), (3, 1), (5, 0), (5, 1), (7, 0), (7, 1), (9, 0), (9, 1), (11, 0), (11, 1), (13, 0), (13, 1), (15, 0), (15, 1), (17, 0), (17, 1), (18, 0), (18, 1), (19, 0), (19, 1))
-VP = (2, 2, 2, 2, 1, 1, 1, 1, 0, 0, 0, 0, 0, 0, 0, 0)
+S_PAIR = ((5, 0), (5, 1), (7, 0), (7, 1), (9, 0), (9, 1), (11, 0), (11, 1), (13, 0), (13, 1), (14, 0), (14, 1), (15, 0), (15, 1), (17, 0), (17, 1), (18, 0), (18, 1), (19, 0), (19, 1))
+VP = (2, 2, 2, 2, 0, 0, 0, 0, 0, 0, 0, 0, 0, 0, 0, 0)
 VW = 1
 W_POS = 1
+M_END = 1
 ADD_LAST = 99
 CST_S = 0
 XB = 2
@@ -44,7 +45,7 @@ MIX_AT = 4
 TURN_AT = 3
 SWAP_AT = 3
 CST_AT = 4
-LOADS = ('s0', 'a0', 'b0', 's1', 'w1', 's2', 'w2', 'x0', 's3', 'w3', 'x1', 'w4', 'x2', 'c', 'w5', 'g', 'x3')
+LOADS = ('s0', 'a0', 'b0', 's1', 'w1', 's2', 'w2', 'x0', 's3', 'w3', 'x1', 'w4', 'x2', 'w5', 'w6', 'c', 'g', 'x3')
 TABLE_MM = (5, 6, 7, 8)
 L_MX = 5
 L_ST = 5
@@ -132,6 +133,12 @@ def tile_gqa_flashattn_pa_kernel(
             nc.sync.dma_start(out=t[:], in_=x[0, i * P : (i + 1) * P, :])
             xr[i] = t
 
+        def load_half_x(i, half):
+            if half == 0:
+                xr[i] = x_pool.tile([P, 2048], BF16, name="xraw", tag="xraw")
+            lo = 1024 * half
+            nc.sync.dma_start(out=xr[i][:, lo : lo + 1024], in_=x[0, i * P : (i + 1) * P, lo : lo + 1024])
+
         gcol = const.tile([P, 4, 16], BF16, name="gcol", tag="gcol")
         cs = const.tile([P, 2, NT, HD], BF16, name="cs", tag="cs")
 
@@ -151,6 +158,8 @@ def tile_gqa_flashattn_pa_kernel(
                 load_vectors()
             elif what == "c":
                 load_cos_sin()
+            elif what[0] in "yz":
+                load_half_x(int(what[1]), "yz".index(what[0]))
             elif what[0] in "ab":
                 load_half_chunk(int(what[1]), "ab".index(what[0]))
             elif what[0] == "s":
@@ -510,9 +519,9 @@ def tile_gqa_flashattn_pa_kernel(
             for e in full:
                 copy_values(e)
             full.clear()
-            if s == MIX_AT:
+            if s == MIX_AT and not M_END:
                 mix_matrices()
-            if s == CST_AT and not CST_S:
+            if s == CST_AT and not CST_S and not M_END:
                 copy_cos_sin()
             if W_POS == 0 and 0 <= s + VW < NCHUNK:
                 vector_widen(s + VW)
@@ -537,6 +546,10 @@ def tile_gqa_flashattn_pa_kernel(
                 quantize(s - 1)
             if W_POS == 3 and 0 <= s + VW < NCHUNK:
                 vector_widen(s + VW)
+            if s == MIX_AT and M_END:
+                mix_matrices()
+            if s == CST_AT and not CST_S and M_END:
+                copy_cos_sin()
             for e in units(s, L_ST):
                 for j in range(2):
                     if (e, j) not in S_PAIR:

@@ -26,11 +26,12 @@ NCHUNK = 24
 NNORM = 20
 SA = 2
 S_INTER = (10, 14, 16, 17, 18, 19, 20, 21, 22, 23)
-V_ADD = (10, 13, 16, 17, 18, 19)
-S_PAIR = ((5, 0), (5, 1), (7, 0), (7, 1), (9, 0), (9, 1), (11, 0), (11, 1), (13, 0), (13, 1), (14, 0), (14, 1), (15, 0), (15, 1), (17, 0), (17, 1), (18, 0), (18, 1), (19, 0), (19, 1))
+V_ADD = (7, 10, 13, 16, 17, 18, 19)
+S_PAIR = ((5, 0), (5, 1), (7, 0), (7, 1), (9, 0), (9, 1), (11, 0), (11, 1), (13, 0), (13, 1), (15, 0), (15, 1), (17, 0), (17, 1), (18, 0), (18, 1), (19, 0), (19, 1))
 VP = (2, 2, 2, 2, 0, 0, 0, 0, 0, 0, 0, 0, 0, 0, 0, 0)
 VW = 1
 W_POS = 1
+G_ADD = (7, 10, 13, 16)
 M_END = 1
 ADD_LAST = 99
 CST_S = 0
@@ -45,7 +46,7 @@ MIX_AT = 4
 TURN_AT = 3
 SWAP_AT = 3
 CST_AT = 4
-LOADS = ('s0', 'a0', 'b0', 's1', 'w1', 's2', 'w2', 'x0', 's3', 'w3', 'x1', 'w4', 'x2', 'w5', 'w6', 'c', 'g', 'x3')
+LOADS = ('s0', 'a0', 'b0', 's1', 'w1', 's2', 'w2', 'y0', 'z0', 's3', 'w3', 'x1', 'w4', 'x2', 'w5', 'w6', 'c', 'g', 'x3')
 TABLE_MM = (5, 6, 7, 8)
 L_MX = 5
 L_ST = 5
@@ -441,6 +442,17 @@ def tile_gqa_flashattn_pa_kernel(
             )
             sums[e] = cc
 
+        def gpsimd_add(e):
+            ab = work[e]
+            cc = c_pool.tile([P, 4, HD], F32, name="cc", tag="cc")
+            nc.gpsimd.tensor_tensor(
+                out=cc[:].rearrange("p h (a d) -> p h a d", a=2),
+                in0=ab[:, :, 1, :].rearrange("p h (a d) -> p h a d", a=2),
+                in1=ab[:, :, 0, :].rearrange("p h (a d) -> p h a d", a=2)[:, :, ::-1, :],
+                op=ALU.add,
+            )
+            sums[e] = cc
+
         def out_view(e):
             kind, idx = GROUPS[e // NT]
             i = e % NT
@@ -526,7 +538,9 @@ def tile_gqa_flashattn_pa_kernel(
             if W_POS == 0 and 0 <= s + VW < NCHUNK:
                 vector_widen(s + VW)
             for e in units(s, L_ADD):
-                if e in V_ADD:
+                if e in V_ADD and e in G_ADD:
+                    gpsimd_add(e)
+                elif e in V_ADD:
                     vector_add(e)
             if 1 <= s <= NCHUNK:
                 interleave(s - 1)

from contextlib import ExitStack

import concourse.mybir as mybir
from concourse.masks import make_identity

F32 = mybir.dt.float32
BF16 = mybir.dt.bfloat16
U32 = mybir.dt.uint32
U8 = mybir.dt.uint8
FP8 = mybir.dt.float8_e4m3fn
FP8X4 = mybir.dt.float8_e4m3fn_x4
ALU = mybir.AluOpType
ACT = mybir.ActivationFunctionType

P = 128
HD = 128
HALF = 64
NT = 4
NG = 4
GW = 512
EPS = 1e-6
FLOPS = 2 * 512 * 2048 * 3072

GROUPS = (("q", 0), ("q", 1), ("q", 2), ("q", 3), ("k", 0), ("v", 0))
NCHUNK = 24
NNORM = 20
SA = 2
S_INTER = (10, 14, 16, 17, 18, 19, 20, 21, 22, 23)
V_ADD = (7, 10, 13, 16, 17, 18, 19)
S_PAIR = ((5, 0), (5, 1), (7, 0), (7, 1), (9, 0), (9, 1), (11, 0), (11, 1), (13, 0), (13, 1), (15, 0), (15, 1), (17, 0), (17, 1), (18, 0), (18, 1), (19, 0), (19, 1))
VP = (2, 2, 2, 2, 0, 0, 0, 0, 0, 0, 0, 0, 0, 0, 0, 0)
VW = 1
W_POS = 1
G_ADD = (7, 10, 13, 16)
M_END = 1
ADD_LAST = 99
CST_S = 0
XB = 2
XN = 4
SPLIT_FROM = 19
G_INTER = ()
G_PIECES = 4
G_AHEAD = 0
X_STEP = (0, 1, 2, 4)
MIX_AT = 4
TURN_AT = 3
SWAP_AT = 3
CST_AT = 4
LOADS = ('s0', 'a0', 'b0', 's1', 'w1', 's2', 'w2', 'y0', 'z0', 's3', 'w3', 'x1', 'w4', 'x2', 'w5', 'w6', 'c', 'g', 'x3')
TABLE_MM = (5, 6, 7, 8)
L_MX = 5
L_ST = 5
L_AB = 7
L_ADD = 8
L_FIN = 10
L_FINV = 10
EARLY = ()
FIN_EARLY = (16, 17, 18, 19)


def v_planes(s):
    return tuple(range(4 - VP[s], 4)) if s < len(VP) and GROUPS[s // NG][0] == "q" else ()


def tile_gqa_flashattn_pa_kernel(
    tc, x, cos, sin, wq_bytes, wq_scale, wk, wv, q_gamma, q_beta, k_gamma, k_beta, out_q, out_k, out_v
):
    nc = tc.nc
    with ExitStack() as ctx:
        const = ctx.enter_context(tc.tile_pool(name="const", bufs=1))
        bytes_pool = ctx.enter_context(tc.tile_pool(name="bytes", bufs=16))
        raw_pool = ctx.enter_context(tc.tile_pool(name="raw", bufs=8))
        x_pool = ctx.enter_context(tc.tile_pool(name="xraw", bufs=4))
        gx_pool = ctx.enter_context(tc.tile_pool(name="gx", bufs=4))
        wide_pool = ctx.enter_context(tc.tile_pool(name="wide", bufs=6))
        grp_pool = ctx.enter_context(tc.tile_pool(name="grp", bufs=5))
        code_pool = ctx.enter_context(tc.tile_pool(name="codes", bufs=10))
        stat_pool = ctx.enter_context(tc.tile_pool(name="stats", bufs=6))
        junk_pool = ctx.enter_context(tc.tile_pool(name="junk", bufs=4))
        inv_pool = ctx.enter_context(tc.tile_pool(name="inv", bufs=6))
        ab_pool = ctx.enter_context(tc.tile_pool(name="ab", bufs=3))
        c_pool = ctx.enter_context(tc.tile_pool(name="cc", bufs=4))
        o_pool = ctx.enter_context(tc.tile_pool(name="o", bufs=8))
        psum = ctx.enter_context(tc.psum_pool(name="psum", bufs=1))
        ctx.enter_context(tc.manual_schedule())

        one = const.tile([P, 1], F32, name="one", tag="one")
        nc.gpsimd.memset(one[:], 1.0)
        warm = const.tile([P, 1], F32, name="warm", tag="warm")
        nc.scalar.activation(out=warm[:], in_=one[:], func=ACT.Abs_reciprocal_sqrt)
        rmat = const.tile([P, 3, P], BF16, name="rmat", tag="rmat")
        make_identity(nc, rmat[:, 0, :])
        nc.gpsimd.tensor_copy(out=rmat[:, 1, 0:HALF], in_=rmat[:, 0, HALF:P])
        nc.gpsimd.tensor_copy(out=rmat[:, 1, HALF:P], in_=rmat[:, 0, 0:HALF])
        nc.gpsimd.tensor_scalar(
            out=rmat[:, 2, 0:HALF], in0=rmat[:, 0, HALF:P], scalar1=-1.0, scalar2=0.0, op0=ALU.mult, op1=ALU.add
        )
        nc.gpsimd.tensor_copy(out=rmat[:, 2, HALF:P], in_=rmat[:, 0, 0:HALF])
        ident = const.tile([P, P], F32, name="ident", tag="ident")
        make_identity(nc, ident[:])

        wsc = const.tile([P, NG, 8], F32, name="wsc", tag="wsc")
        wsc_v = wq_scale.rearrange("(g p t) o -> g p (t o)", p=P, t=4)

        def load_scales(g):
            nc.sync.dma_start(out=wsc[:, g, 0:4], in_=wsc_v[g])

        wq_v = wq_bytes.rearrange("(g p t) n -> g p t n", p=P, t=4)
        wk_v = wk.rearrange("(g p t) n -> g p t n", p=P, t=4)
        wv_v = wv.rearrange("(g p t) n -> g p t n", p=P, t=4)
        raw = {}
        xr = {}

        def load_chunk(s):
            kind, idx = GROUPS[s // NG]
            g = s % NG
            if kind == "q":
                t = bytes_pool.tile([P, 4, GW], U8, name="wq_bytes", tag="wq_bytes")
                nc.sync.dma_start(out=t[:], in_=wq_v[g][:, :, idx * GW : (idx + 1) * GW])
            else:
                t = raw_pool.tile([P, 4, GW], BF16, name="wkv_raw", tag="wkv_raw")
                nc.sync.dma_start(out=t[:], in_=(wk_v if kind == "k" else wv_v)[g])
            raw[s] = t

        def load_half_chunk(s, half):
            if half == 0:
                raw[s] = bytes_pool.tile([P, 4, GW], U8, name="wq_bytes", tag="wq_bytes")
            nc.sync.dma_start(
                out=raw[s][:, 2 * half : 2 * half + 2, :], in_=wq_v[s % NG][:, 2 * half : 2 * half + 2, 0:GW]
            )

        def load_x(i):
            t = x_pool.tile([P, 2048], BF16, name="xraw", tag="xraw")
            nc.sync.dma_start(out=t[:], in_=x[0, i * P : (i + 1) * P, :])
            xr[i] = t

        def load_half_x(i, half):
            if half == 0:
                xr[i] = x_pool.tile([P, 2048], BF16, name="xraw", tag="xraw")
            lo = 1024 * half
            nc.sync.dma_start(out=xr[i][:, lo : lo + 1024], in_=x[0, i * P : (i + 1) * P, lo : lo + 1024])

        gcol = const.tile([P, 4, 16], BF16, name="gcol", tag="gcol")
        cs = const.tile([P, 2, NT, HD], BF16, name="cs", tag="cs")

        def load_vectors():
            v = 0
            with nc.allow_non_contiguous_dma(reason="four vectors of 128 values, one value to a partition"):
                for vec in (q_gamma, k_gamma, q_beta, k_beta):
                    nc.sync.dma_start(out=gcol[:, v, 0:1], in_=vec.rearrange("(p o) -> p o", o=1))
                    v += 1

        def load_cos_sin():
            nc.sync.dma_start(out=cs[:, 0, :, :], in_=cos.rearrange("(i p) d -> p i d", p=P))
            nc.sync.dma_start(out=cs[:, 1, :, :], in_=sin.rearrange("(i p) d -> p i d", p=P))

        for what in LOADS:
            if what == "g":
                load_vectors()
            elif what == "c":
                load_cos_sin()
            elif what[0] in "yz":
                load_half_x(int(what[1]), "yz".index(what[0]))
            elif what[0] in "ab":
                load_half_chunk(int(what[1]), "ab".index(what[0]))
            elif what[0] == "s":
                load_scales(int(what[1]))
            elif what[0] == "x":
                load_x(int(what[1]))
            else:
                load_chunk(int(what[1]))
        for s in range(NCHUNK):
            if s not in raw:
                load_chunk(s)

        ab_t = const.tile([P, NT, 2, 2, HD], F32, name="ab_t", tag="ab_t")
        c_t = const.tile([P, NT, 2, HD], F32, name="c_t", tag="c_t")
        mix = const.tile([P, 4, 2, HD], BF16, name="mix", tag="mix")
        cst = const.tile([P, 2, NT, HD], BF16, name="cst", tag="cst")
        turned = []
        swapped = []

        def turn_cos_sin():
            ps = psum.tile([P, 2, NT, P], BF16, name="csp", tag="b6")
            for w in range(2):
                for i in range(NT):
                    nc.tensor.transpose(ps[:, w, i, :], cs[:, w, i, :], rmat[:, 0, :])
            turned.append(ps)

        def swap_vectors():
            swp = psum.tile([P, 4], F32, name="swp", tag="b7")
            nc.tensor.matmul(out=swp[:], lhsT=rmat[:, 2, :], rhs=gcol[:, :, 0], start=True, stop=True)
            swapped.append(swp)

        def mix_matrices():
            swp = swapped[0]
            for k in range(2):
                for j, block, col in (
                    (1, 0, gcol[:, k, 0:1]), (2, 0, gcol[:, 2 + k, 0:1]), (0, 1, swp[:, k : k + 1]), (3, 0, swp[:, 2 + k : 3 + k])
                ):
                    nc.vector.tensor_scalar(
                        out=mix[:, j, k, :], in0=rmat[:, block, :], scalar1=col, scalar2=None, op0=ALU.mult
                    )

        def copy_cos_sin():
            (nc.scalar.copy if CST_S else nc.vector.tensor_copy)(out=cst[:].rearrange("p w i d -> p (w i d)"), in_=turned[0][:].rearrange("p w i d -> p (w i d)"))

        tab_ps = {}

        def table_matmuls(i):
            ab = psum.tile([P, 2, 2, HD], F32, name="tab", tag="b6")
            c = psum.tile([P, 2, HD], F32, name="tc", tag="b7")
            nc.tensor.matmul(out=ab[:, 1, :, :], lhsT=cst[:, 0, i, :], rhs=mix[:, 1, :, :], start=True, stop=True)
            nc.tensor.matmul(out=ab[:, 0, :, :], lhsT=cst[:, 1, i, :], rhs=mix[:, 0, :, :], start=True, stop=True)
            nc.tensor.matmul(out=c[:], lhsT=cst[:, 0, i, :], rhs=mix[:, 2, :, :], start=True, stop=False)
            nc.tensor.matmul(out=c[:], lhsT=cst[:, 1, i, :], rhs=mix[:, 3, :, :], start=False, stop=True)
            tab_ps[i] = (ab, c)

        def table_copies(i):
            def run_ab():
                nc.scalar.copy(out=ab_t[:, i, :, :, :].rearrange("p k w d -> p w k d"), in_=tab_ps[i][0][:])

            def run_c():
                nc.scalar.copy(out=c_t[:, i, :, :], in_=tab_ps[i][1][:])
            return [run_ab, run_c]

        xc = const.tile([P, NT * NG * P], U32, name="xc", tag="xc", align_bytes=64)
        xs = const.tile([P, NT * NG * P], U8, name="xs", tag="xs", align_bytes=64)
        gxs = {}

        def x_turn(i, half):
            def run():
                words = xr[i][:].bitcast(F32)
                xt = psum.tile([P, 2, 2, P], F32, name="xt", tag="b%d" % (XB + (2 * i + half) % XN))
                for gl in range(2):
                    g = 2 * half + gl
                    for u in range(2):
                        nc.tensor.transpose(xt[:, gl, u, :], words[:, 256 * g + u : 256 * (g + 1) : 2], ident[:])
                if half == 0:
                    gxs[i] = gx_pool.tile([P, NG, P, 4], BF16, name="gx", tag="gx", align_bytes=64)
                dst = gxs[i][:, 2 * half : 2 * half + 2, :, :].rearrange("p g r j -> p (g r j)").bitcast(F32)
                nc.scalar.copy(
                    out=dst.rearrange("p (g r u) -> p g r u", g=2, u=2), in_=xt[:].rearrange("p g u r -> p g r u")
                )
            return run

        def x_quant(i):
            lo = NG * i * P
            nc.vector.quantize_mx(
                out=xc[:, lo : lo + NG * P].bitcast(FP8X4),
                scales=xs[:, lo : lo + NG * P],
                in_=gxs[i][:].rearrange("p g r j -> p (g r j)"),
            )

        wides = {}
        grps = {}
        codes = {}

        def widen_plane(s, t):
            def run():
                g = s % NG
                nc.scalar.activation(
                    out=wides[s][:, t, :], in_=raw[s][:, t, :].bitcast(FP8), func=ACT.Copy,
                    scale=wsc[:, g, t : t + 1],
                )
            return run

        def scalar_interleave(s):
            def run():
                src = wides[s] if GROUPS[s // NG][0] == "q" else raw[s]
                nc.scalar.copy(
                    out=grps[s][:].rearrange("p (c i) t -> p c t i", i=4),
                    in_=src[:].rearrange("p t (c i) -> p c t i", i=4),
                )
            return run

        def prep_scalar_ops(s):
            ops = []
            if s - 1 in S_INTER:
                grps[s - 1] = grp_pool.tile([P, GW, 4], BF16, name="grp", tag="grp", align_bytes=64)
                ops.append(scalar_interleave(s - 1))
            if s < NCHUNK and GROUPS[s // NG][0] == "q":
                wides[s] = wide_pool.tile([P, 4, GW], BF16, name="wide", tag="wide")
                ops.extend([widen_plane(s, t) for t in range(4) if t not in v_planes(s)])
            for i in range(NT):
                if X_STEP[i] == s - SA:
                    ops.extend([x_turn(i, half) for half in range(2)])
            return ops

        def vector_widen(s):
            g = s % NG
            for t in v_planes(s):
                nc.vector.tensor_scalar(
                    out=wides[s][:, t, :], in0=raw[s][:, t, :].bitcast(FP8), scalar1=wsc[:, g, t : t + 1],
                    scalar2=None, op0=ALU.mult,
                )

        def gpsimd_interleave(s):
            src = wides[s] if GROUPS[s // NG][0] == "q" else raw[s]
            grps[s] = grp_pool.tile([P, GW, 4], BF16, name="grp", tag="grp", align_bytes=64)
            w = GW // G_PIECES
            for c in range(G_PIECES):
                nc.gpsimd.tensor_scalar(
                    out=grps[s][:, c * w : (c + 1) * w, :], in0=src[:, :, c * w : (c + 1) * w].rearrange("p t n -> p n t"),
                    scalar1=1.0, scalar2=0.0, op0=ALU.mult, op1=ALU.add,
                )

        def interleave(s):
            if s in S_INTER or s in G_INTER:
                return
            src = wides[s] if GROUPS[s // NG][0] == "q" else raw[s]
            grps[s] = grp_pool.tile([P, GW, 4], BF16, name="grp", tag="grp", align_bytes=64)
            nc.vector.tensor_copy(
                out=grps[s][:].rearrange("p (c i) t -> p c t i", i=4), in_=src[:].rearrange("p t (c i) -> p c t i", i=4)
            )

        def quantize(s):
            wc = code_pool.tile([P, GW], U32, name="wc", tag="wc", align_bytes=64)
            ws = code_pool.tile([P, GW], U8, name="ws", tag="ws", align_bytes=64)
            nc.vector.quantize_mx(
                out=wc[:].bitcast(FP8X4), scales=ws[:], in_=grps[s][:].rearrange("p n t -> p (n t)")
            )
            codes[s] = (wc, ws)

        accs = {}
        stats = {}
        invs = {}
        work = {}
        sums = {}

        def unit_matmuls(e):
            c = e // NT
            i = e % NT
            acc = psum.tile([P, GW], F32, name="acc", tag="b%d" % (e % 4 + (4 if e >= NNORM else 0)))
            for g in range(NG):
                wc, ws = codes[NG * c + g]
                lo = (NG * i + g) * P
                nc.tensor.matmul_mx(
                    out=acc[:],
                    lhsT=xc[:, lo : lo + P].bitcast(FP8X4),
                    lhsT_scale=xs[:, lo : lo + P],
                    rhs=wc[:].bitcast(FP8X4),
                    rhs_scale=ws[:],
                    start=(g == 0),
                    stop=(g == NG - 1),
                )
            accs[e] = acc

        def value_start_step(e):
            users = [n for n in range(NNORM) if n % 4 == e % 4 and n not in V_ADD]
            return max(users + [0]) + L_FIN + 1

        def value_passes(e, g_lo, g_hi):
            c = e // NT
            i = e % NT
            if e not in accs:
                accs[e] = psum.tile([P, GW], F32, name="acc", tag="b%d" % (4 + e % 4))
            for g in range(g_lo, g_hi):
                wc, ws = codes[NG * c + g]
                lo = (NG * i + g) * P
                nc.tensor.matmul_mx(
                    out=accs[e][:],
                    lhsT=xc[:, lo : lo + P].bitcast(FP8X4),
                    lhsT_scale=xs[:, lo : lo + P],
                    rhs=wc[:].bitcast(FP8X4),
                    rhs_scale=ws[:],
                    start=(g == 0),
                    stop=(g == NG - 1),
                )

        def vector_stats(e, j):
            nc.vector.bn_stats(
                out=stats[e][:, j, :, :].rearrange("p e c -> p (e c)"),
                in_=accs[e][:, 2 * j * HD : 2 * (j + 1) * HD].rearrange("p (e d) -> p d e", e=2),
            )

        def head_sum(e, h):
            def run():
                junk = junk_pool.tile([P, HD], BF16, name="junk", tag="junk")
                nc.scalar.activation(
                    out=junk[:], in_=accs[e][:, h * HD : (h + 1) * HD], func=ACT.Identity, scale=-1.0 / HD,
                    accum_out=stats[e][:, h // 2, h % 2, 1:2],
                )
            return run

        def head_sq(e, h):
            def run():
                junk = junk_pool.tile([P, HD], BF16, name="junk", tag="junk")
                nc.scalar.activation(
                    out=junk[:], in_=accs[e][:, h * HD : (h + 1) * HD], func=ACT.Square,
                    bias=stats[e][:, h // 2, h % 2, 1:2], accum_out=stats[e][:, h // 2, h % 2, 2:3],
                )
            return run

        def scalar_stats(e):
            heads = [h for h in range(4) if (e, h // 2) in S_PAIR]
            return [head_sum(e, h) for h in heads], [head_sq(e, h) for h in heads]

        def inv_std(e):
            def run():
                inv = inv_pool.tile([P, 4], F32, name="inv", tag="inv")
                nc.scalar.activation(
                    out=inv[:].rearrange("p (j e) -> p j e", j=2), in_=stats[e][:, :, :, 2], func=ACT.Abs_reciprocal_sqrt,
                    scale=1.0 / HD, bias=EPS,
                )
                invs[e] = inv
            return run

        def epi_ab(e):
            kind = ("q", "k").index(GROUPS[e // NT][0])
            i = e % NT
            ab = ab_pool.tile([P, 4, 2, HD], F32, name="ab", tag="ab")
            for h in (3, 2, 1, 0):
                nc.vector.scalar_tensor_tensor(
                    out=ab[:, h, :, :],
                    in0=accs[e][:, h * HD : (h + 1) * HD].unsqueeze(1).to_broadcast([P, 2, HD]),
                    scalar=stats[e][:, h // 2, h % 2, 1:2],
                    in1=ab_t[:, i, kind, :, :],
                    op0=ALU.add if (e, h // 2) in S_PAIR else ALU.subtract,
                    op1=ALU.mult,
                )
            work[e] = ab

        def tensor_add(e):
            ab = work[e]
            cps = psum.tile([P, 4, HD], F32, name="cps", tag="b%d" % (4 + e % 4))
            nc.tensor.matmul(out=cps[:], lhsT=ident[:], rhs=ab[:, :, 1, :], start=True, stop=False)
            nc.tensor.matmul(
                out=cps[:].rearrange("p h (a d) -> p h a d", a=2), lhsT=ident[:],
                rhs=ab[:, :, 0, :].rearrange("p h (a d) -> p h a d", a=2)[:, :, ::-1, :], start=False, stop=True,
            )
            sums[e] = cps

        def vector_add(e):
            ab = work[e]
            cc = c_pool.tile([P, 4, HD], F32, name="cc", tag="cc")
            nc.vector.tensor_tensor(
                out=cc[:].rearrange("p h (a d) -> p h a d", a=2),
                in0=ab[:, :, 1, :].rearrange("p h (a d) -> p h a d", a=2),
                in1=ab[:, :, 0, :].rearrange("p h (a d) -> p h a d", a=2)[:, :, ::-1, :],
                op=ALU.add,
            )
            sums[e] = cc

        def gpsimd_add(e):
            ab = work[e]
            cc = c_pool.tile([P, 4, HD], F32, name="cc", tag="cc")
            nc.gpsimd.tensor_tensor(
                out=cc[:].rearrange("p h (a d) -> p h a d", a=2),
                in0=ab[:, :, 1, :].rearrange("p h (a d) -> p h a d", a=2),
                in1=ab[:, :, 0, :].rearrange("p h (a d) -> p h a d", a=2)[:, :, ::-1, :],
                op=ALU.add,
            )
            sums[e] = cc

        def out_view(e):
            kind, idx = GROUPS[e // NT]
            i = e % NT
            dram = out_q if kind == "q" else (out_k if kind == "k" else out_v)
            return dram[0, 4 * idx : 4 * idx + 4, i * P : (i + 1) * P, :].rearrange("h p d -> p h d")

        def final(e):
            kind = ("q", "k").index(GROUPS[e // NT][0])
            i = e % NT
            o = o_pool.tile([P, 4, HD], F32, name="o", tag="o")
            for h in range(4):
                nc.vector.scalar_tensor_tensor(
                    out=o[:, h, :], in0=sums[e][:, h, :], scalar=invs[e][:, h : h + 1], in1=c_t[:, i, kind, :],
                    op0=ALU.mult, op1=ALU.add,
                )
                if e >= SPLIT_FROM and h % 2 == 1:
                    nc.sync.dma_start(out=out_view(e)[:, h - 1 : h + 1, :], in_=o[:, h - 1 : h + 1, :])
            if e < SPLIT_FROM:
                nc.sync.dma_start(out=out_view(e), in_=o[:])

        def copy_values(e):
            o = o_pool.tile([P, 4, HD], F32, name="o", tag="o")
            nc.scalar.copy(out=o[:].rearrange("p h d -> p (h d)"), in_=accs[e][:])
            nc.sync.dma_start(out=out_view(e), in_=o[:])

        def normed(e):
            return 0 <= e < NNORM

        def units(s, lag):
            return [e for e in range(NNORM) if e - (1 if e in EARLY else 0) + lag == s]

        done = {e: 0 for e in range(NNORM, NCHUNK)}
        full = []
        for s in range(-SA, NCHUNK + L_FIN + 2):
            for e in units(s, L_MX):
                unit_matmuls(e)
            for e in units(s, L_ADD):
                if e not in V_ADD and s < ADD_LAST:
                    tensor_add(e)
            if s in TABLE_MM:
                table_matmuls(TABLE_MM.index(s))
            for e in range(NNORM, NCHUNK):
                ready = min(NG, s - (NNORM + 1))
                if s >= value_start_step(e) and ready > done[e]:
                    value_passes(e, done[e], ready)
                    done[e] = ready
                    if ready == NG:
                        full.append(e)
            for e in units(s, L_ADD):
                if e not in V_ADD and s >= ADD_LAST:
                    tensor_add(e)
            fill = prep_scalar_ops(s + SA) if s + SA <= NCHUNK else []
            seq = fill[0:1]
            for e in units(s, L_ADD):
                seq.append(inv_std(e))
            seq.extend(fill[1:2])
            sums_ops, sq_ops = [], []
            for e in units(s, L_ST):
                stats[e] = stat_pool.tile([P, 2, 2, 3], F32, name="st", tag="st")
                a_ops, b_ops = scalar_stats(e)
                sums_ops.extend(a_ops)
                sq_ops.extend(b_ops)
            seq.extend(sums_ops + fill[2:4] + sq_ops + fill[4:])
            if s in TABLE_MM:
                seq.extend(table_copies(TABLE_MM.index(s)))
            if s == SWAP_AT:
                swap_vectors()
            for op in seq:
                op()
            if s == CST_AT and CST_S:
                copy_cos_sin()
            if s + G_AHEAD in G_INTER:
                gpsimd_interleave(s + G_AHEAD)
            if s == TURN_AT:
                turn_cos_sin()
            for e in full:
                copy_values(e)
            full.clear()
            if s == MIX_AT and not M_END:
                mix_matrices()
            if s == CST_AT and not CST_S and not M_END:
                copy_cos_sin()
            if W_POS == 0 and 0 <= s + VW < NCHUNK:
                vector_widen(s + VW)
            for e in units(s, L_ADD):
                if e in V_ADD and e in G_ADD:
                    gpsimd_add(e)
                elif e in V_ADD:
                    vector_add(e)
            if 1 <= s <= NCHUNK:
                interleave(s - 1)
            if W_POS == 1 and 0 <= s + VW < NCHUNK:
                vector_widen(s + VW)
            for i in range(NT):
                if X_STEP[i] + 2 == s:
                    x_quant(i)
            for e in range(NNORM):
                if e + (L_FINV if e in V_ADD else L_FIN) - (1 if e in FIN_EARLY else 0) == s:
                    final(e)
            for e in units(s, L_AB):
                epi_ab(e)
            if W_POS == 2 and 0 <= s + VW < NCHUNK:
                vector_widen(s + VW)
            if 1 <= s <= NCHUNK:
                quantize(s - 1)
            if W_POS == 3 and 0 <= s + VW < NCHUNK:
                vector_widen(s + VW)
            if s == MIX_AT and M_END:
                mix_matrices()
            if s == CST_AT and not CST_S and M_END:
                copy_cos_sin()
            for e in units(s, L_ST):
                for j in range(2):
                    if (e, j) not in S_PAIR:
                        vector_stats(e, j)
